import numpy as np
import ml_dtypes


def mxq(x, axis, fmt="e4m3"):
    dtype, down = {"e4m3": (ml_dtypes.float8_e4m3fn, 7), "e5m2": (ml_dtypes.float8_e5m2, 14)}[fmt]
    v = np.moveaxis(np.asarray(x, np.float32).astype(ml_dtypes.bfloat16).astype(np.float64), axis, -1)
    blocks = v.reshape(v.shape[:-1] + (-1, 32))
    amax = np.abs(blocks).max(-1, keepdims=True)
    byte = np.maximum(np.where(amax > 0, np.frexp(amax)[1] - 1 + 127, 0) - down, 1)
    scale = np.exp2(byte - 127.0)
    codes = (blocks / scale).astype(np.float32).astype(dtype).astype(np.float64)
    return np.moveaxis((codes * scale).reshape(v.shape), -1, axis)


WIDE = False


def mx_kscale(k):
    if not WIDE:
        return np.ones(k)
    levels = np.array([10, -10, 5, -5, 0])
    a = np.random.permutation(np.resize(levels, k // 512 * 4)).reshape(k // 512, 4)
    idx = np.arange(k)
    return np.exp2(a[idx // 512, idx % 128 // 32])


BF16 = ml_dtypes.bfloat16


def bf(x):
    return np.asarray(x, np.float32).astype(BF16)


def f64(x):
    return np.asarray(x).astype(np.float64)


E2M1 = np.array([0.0, 0.5, 1.0, 1.5, 2.0, 3.0, 4.0, 6.0, -0.0, -0.5, -1.0, -1.5, -2.0, -3.0, -4.0, -6.0])


def pack_weight(w, fmt):
    k, n = w.shape
    w = f64(bf(w)).reshape(k // 32, 32, n)
    amax = np.abs(w).max(1)
    if fmt == "e4m3":
        byte = np.frexp(amax)[1] - 1 + 127 - 7
    else:
        mant, ex = np.frexp(amax / 6.0)
        byte = np.where(mant > 0.5, ex, ex - 1) + 127
    byte = np.clip(np.where(amax > 0, byte, 1), 1, 254)
    scaled = (w * np.exp2(127.0 - byte)[:, None, :]).reshape(k, n).astype(np.float32)
    by_word = np.ascontiguousarray(scaled.reshape(k // 512, 128, 4, n).transpose(0, 1, 3, 2))
    if fmt == "e4m3":
        words = by_word.astype(ml_dtypes.float8_e4m3fn).view(np.uint8)
    else:
        c = by_word.astype(ml_dtypes.float4_e2m1fn).view(np.uint8) & 0xF
        words = c[..., 0::2] | (c[..., 1::2] << 4)
    return np.ascontiguousarray(words), np.ascontiguousarray(byte.astype(np.uint8).reshape(k // 512, 16, n))


def unpack_weight(words, scales, fmt):
    g, p, n, _ = words.shape
    if fmt == "e4m3":
        vals = np.ascontiguousarray(words).view(ml_dtypes.float8_e4m3fn).astype(np.float64)
    else:
        nib = np.empty((g, p, n, 4), np.uint8)
        nib[..., 0::2] = words & 0xF
        nib[..., 1::2] = words >> 4
        vals = E2M1[nib]
    vals = vals * np.repeat(np.exp2(scales.astype(np.float64) - 127.0), 8, axis=1)[..., None]
    return vals.transpose(0, 1, 3, 2).reshape(g * 512, n)


BATCH, S, D_IN, Q, K, D_OUT = 2, 64, 512, 8192, 2, 512
QK = Q * K
FMT = "e4m3"


def setup_inputs():
    s = mx_kscale(D_IN)
    lim = 1.0 / np.sqrt(D_IN)
    X0 = bf(np.random.standard_normal((BATCH, S, D_IN)) * s)
    t = bf(np.random.uniform(0.2, 1.0, (BATCH, 1)))
    wc = np.random.uniform(-lim, lim, (Q, D_IN)) / s
    words, scales = pack_weight(np.ascontiguousarray(wc.T), FMT)
    return {"X0": X0,
            "t": t,
            "Wc_w_words": words,
            "Wc_w_scales": scales,
            "Wc_b": bf(np.random.standard_normal(Q) * 0.3),
            "w": bf(np.random.standard_normal(Q)),
            "A": bf(np.random.standard_normal((D_OUT, Q, K)) / np.sqrt(QK)),
            "Bp": bf(np.random.uniform(0.0, 2.0 * np.pi, (D_OUT, Q, K)))}


def reference(X0, t, Wc_w_words, Wc_w_scales, Wc_b, w, A, Bp):
    k_vec = np.arange(1.0, K + 1.0)
    C = (mxq(f64(X0), 2, "e4m3") @ unpack_weight(Wc_w_words, Wc_w_scales, FMT)) + f64(Wc_b)
    angle = C + (f64(w)[None, :] * f64(t))[:, None, :]
    angle_k = angle[..., None] * k_vec
    sn = np.sin(angle_k).reshape(BATCH, S, QK)
    cs = np.cos(angle_k).reshape(BATCH, S, QK)
    a_cos = (f64(A) * np.cos(f64(Bp))).reshape(D_OUT, QK)
    a_sin = (f64(A) * np.sin(f64(Bp))).reshape(D_OUT, QK)
    V = ((mxq(sn, 2, "e4m3") @ mxq(a_cos, 1, "e4m3").T)
         + (mxq(cs, 2, "e4m3") @ mxq(a_sin, 1, "e4m3").T))
    return V

@@ -1,0 +1,245 @@
+import math
+
+import concourse.mybir as mybir
+from concourse.masks import make_identity
+
+F32 = mybir.dt.float32
+BF16 = mybir.dt.bfloat16
+I32 = mybir.dt.int32
+U32 = mybir.dt.uint32
+U8 = mybir.dt.uint8
+FP8X4 = mybir.dt.float8_e4m3fn_x4
+ACT = mybir.ActivationFunctionType
+ALU = mybir.AluOpType
+
+P = 128
+PACK = 4
+K_PASS = P * PACK
+D_IN = 512
+Q = 8192
+HARM = 2
+QK = Q * HARM
+D_OUT = 512
+S_LEN = 64
+
+Q_BLOCKS = Q // P
+PASSES = QK // K_PASS
+D_BLOCKS = D_OUT // P
+GROUP = 2
+GROUPS = PASSES // GROUP
+WORDS = K_PASS // HARM
+
+TWO_PI = 2.0 * math.pi
+HALF_PI = 0.5 * math.pi
+
+FLOPS = 2 * P * D_IN * Q + 2 * 2 * P * QK * D_OUT
+
+
+def reduce_angle(nc, pool, x, shape, name):
+    turns = pool.tile([P] + shape, I32, name=name + "_turns")
+    nc.vector.tensor_scalar(out=turns[:], in0=x, scalar1=1.0 / TWO_PI, scalar2=None, op0=ALU.mult)
+    y = pool.tile([P] + shape, F32, name=name + "_y")
+    nc.vector.scalar_tensor_tensor(
+        out=y[:], in0=turns[:], scalar=-TWO_PI, in1=x, op0=ALU.mult, op1=ALU.add
+    )
+    return y
+
+
+def tile_fourierkartlayer_k_kernel(tc, X0, t, Wc_w_words, Wc_w_scales, Wc_b, w, A, Bp, out):
+    nc = tc.nc
+    x0_rows = X0.flatten_outer_dims()
+    w_words = Wc_w_words[0].rearrange("p n t -> p (n t)").bitcast(I32)
+    a_rows = A.rearrange("d q k -> d (q k)")
+    bp_rows = Bp.rearrange("d q k -> d (q k)")
+
+    with tc.tile_pool(name="keep", bufs=1) as keep, tc.tile_pool(name="wload", bufs=4) as wload, tc.tile_pool(
+        name="rows", bufs=2
+    ) as rows, tc.tile_pool(name="load", bufs=3) as load, tc.tile_pool(name="args", bufs=2) as args, tc.tile_pool(
+        name="trig", bufs=2
+    ) as trig, tc.tile_pool(name="codes", bufs=2) as codes, tc.psum_pool(name="ps_acc", bufs=1) as ps_acc, tc.psum_pool(
+        name="ps_a", bufs=2
+    ) as ps_a, tc.psum_pool(name="ps_y", bufs=4) as ps_y, tc.psum_pool(name="ps_c", bufs=1) as ps_c:
+        ident = keep.tile([P, P], F32)
+        make_identity(nc, ident[:])
+        ident_bf = keep.tile([P, P], BF16)
+        make_identity(nc, ident_bf[:])
+
+        w_scales = keep.tile([P, Q], U8, align_bytes=64)
+        nc.vector.memset(w_scales[:].bitcast(I32), 0)
+        for quad in range(4):
+            nc.sync.dma_start(
+                out=w_scales[32 * quad : 32 * quad + 4, :].bitcast(I32),
+                in_=Wc_w_scales[0, 4 * quad : 4 * quad + 4, :].bitcast(I32),
+            )
+        x0_sb = keep.tile([P, D_IN], BF16)
+        nc.sync.dma_start(out=x0_sb[:], in_=x0_rows)
+        bw_rows = keep.tile([P, P], BF16)
+        nc.sync.dma_start(out=bw_rows[0:Q_BLOCKS, :], in_=Wc_b.rearrange("(j p) -> j p", p=P))
+        nc.sync.dma_start(out=bw_rows[Q_BLOCKS:P, :], in_=w.rearrange("(j p) -> j p", p=P))
+        t_bf = keep.tile([P, 2], BF16)
+        nc.sync.dma_start(out=t_bf[:], in_=t.rearrange("b o -> (b o)").partition_broadcast(P))
+        t_f32 = keep.tile([P, 2], F32)
+        nc.vector.tensor_copy(out=t_f32[:], in_=t_bf[:])
+
+        bw_ps = ps_c.tile([P, P], BF16, tag="c")
+        nc.tensor.transpose(bw_ps[:], bw_rows[:], ident_bf[:])
+        bw = keep.tile([P, P], F32)
+        nc.vector.tensor_copy(out=bw[:], in_=bw_ps[:])
+        shift = keep.tile([P, Q_BLOCKS, 2], F32)
+        for b in range(2):
+            nc.vector.scalar_tensor_tensor(
+                out=shift[:, :, b],
+                in0=bw[:, Q_BLOCKS:P],
+                scalar=t_f32[:, b : b + 1],
+                in1=bw[:, 0:Q_BLOCKS],
+                op0=ALU.mult,
+                op1=ALU.add,
+            )
+
+        x0_words = x0_sb[:].bitcast(F32)
+        x0_ps = ps_c.tile([P, P, 2], F32, tag="c")
+        for u in range(2):
+            nc.tensor.transpose(x0_ps[:, :, u], x0_words[:, u : D_IN // 2 : 2], ident[:])
+        x0_grouped = keep.tile([P, P * PACK], BF16, align_bytes=64)
+        nc.vector.tensor_copy(out=x0_grouped[:].bitcast(F32), in_=x0_ps[:].rearrange("p r u -> p (r u)"))
+        x0_codes = keep.tile([P, P], U32, align_bytes=64)
+        x0_scales = keep.tile([P, P], U8, align_bytes=64)
+        nc.vector.quantize_mx(out=x0_codes[:].bitcast(FP8X4), scales=x0_scales[:], in_=x0_grouped[:])
+
+        sin_codes = keep.tile([P, PASSES * P], U32, align_bytes=64)
+        sin_scales = keep.tile([P, PASSES * P], U8, align_bytes=64)
+        cos_codes = keep.tile([P, PASSES * P], U32, align_bytes=64)
+        cos_scales = keep.tile([P, PASSES * P], U8, align_bytes=64)
+        for grp in range(GROUPS):
+            first_block = grp * GROUP * 2
+            w_sb = wload.tile([P, GROUP * 2 * P], U32, align_bytes=64)
+            nc.sync.dma_start(
+                out=w_sb[:].bitcast(I32), in_=w_words[:, first_block * P : (first_block + GROUP * 2) * P]
+            )
+            c_ps = ps_c.tile([P, GROUP * 2, P], F32, tag="c")
+            for blk in range(GROUP * 2):
+                nc.tensor.matmul_mx(
+                    out=c_ps[:, blk, :],
+                    lhsT=w_sb[:, blk * P : (blk + 1) * P].bitcast(FP8X4),
+                    lhsT_scale=w_scales[:, (first_block + blk) * P : (first_block + blk + 1) * P],
+                    rhs=x0_codes[:].bitcast(FP8X4),
+                    rhs_scale=x0_scales[:],
+                    start=True,
+                    stop=True,
+                )
+            k_angle = rows.tile([P, HARM, GROUP, P * 2], F32)
+            for gl in range(GROUP):
+                blocks = slice(2 * gl, 2 * gl + 2)
+                nc.vector.tensor_tensor(
+                    out=k_angle[:, 0, gl, :].rearrange("p (b r u) -> p b r u", b=2, u=2),
+                    in0=c_ps[:, blocks, :].rearrange("p u (b r) -> p b r u", b=2),
+                    in1=shift[:, first_block + 2 * gl : first_block + 2 * gl + 2, :]
+                    .rearrange("p u b -> p b u")
+                    .unsqueeze(2)
+                    .to_broadcast([P, 2, S_LEN, 2]),
+                    op=ALU.add,
+                )
+            nc.vector.tensor_scalar(
+                out=k_angle[:, 1, :, :], in0=k_angle[:, 0, :, :], scalar1=2.0, scalar2=None, op0=ALU.mult
+            )
+            width = GROUP * P * 2
+            y = reduce_angle(nc, rows, k_angle[:].rearrange("p e g c -> p e (g c)"), [HARM, width], "row")
+            y_abs = rows.tile([P, HARM, width], F32)
+            nc.scalar.activation(out=y_abs[:], in_=y[:], func=ACT.Abs)
+            sin_bf = rows.tile([P, width * HARM], BF16, align_bytes=64)
+            nc.scalar.activation(
+                out=sin_bf[:].rearrange("p (c e) -> p c e", e=HARM), in_=y[:].rearrange("p e c -> p c e"), func=ACT.Sin
+            )
+            cos_bf = rows.tile([P, width * HARM], BF16, align_bytes=64)
+            nc.scalar.activation(
+                out=cos_bf[:].rearrange("p (c e) -> p c e", e=HARM),
+                in_=y_abs[:].rearrange("p e c -> p c e"),
+                func=ACT.Sin,
+                scale=-1.0,
+                bias=HALF_PI,
+            )
+            cols = slice(grp * GROUP * P, (grp + 1) * GROUP * P)
+            nc.vector.quantize_mx(out=sin_codes[:, cols].bitcast(FP8X4), scales=sin_scales[:, cols], in_=sin_bf[:])
+            nc.vector.quantize_mx(out=cos_codes[:, cols].bitcast(FP8X4), scales=cos_scales[:, cols], in_=cos_bf[:])
+
+        acc = ps_acc.tile([P, D_OUT], F32)
+        for grp in range(GROUPS):
+            qk_cols = slice(grp * GROUP * K_PASS, (grp + 1) * GROUP * K_PASS)
+            acos_codes = codes.tile([P, GROUP, D_OUT], U32, align_bytes=64)
+            acos_scales = codes.tile([P, GROUP, D_OUT], U8, align_bytes=64)
+            asin_codes = codes.tile([P, GROUP, D_OUT], U32, align_bytes=64)
+            asin_scales = codes.tile([P, GROUP, D_OUT], U8, align_bytes=64)
+            for j in range(D_BLOCKS):
+                d_rows = slice(j * P, (j + 1) * P)
+                bp_sb = load.tile([P, GROUP * K_PASS], BF16)
+                nc.sync.dma_start(out=bp_sb[:], in_=bp_rows[d_rows, qk_cols])
+                a_sb = load.tile([P, GROUP * K_PASS], BF16)
+                nc.sync.dma_start(out=a_sb[:], in_=a_rows[d_rows, qk_cols])
+
+                y = reduce_angle(
+                    nc, args, bp_sb[:].rearrange("p (m e) -> p e m", e=HARM), [HARM, GROUP * WORDS], "phase"
+                )
+
+                a_words = a_sb[:].bitcast(F32)
+                a_ps = ps_a.tile([P, GROUP, P, 2], F32)
+                y_ps = []
+                for gl in range(GROUP):
+                    y_ps.append(ps_y.tile([P, P, PACK], F32, name="y_ps"))
+                    for u in range(2):
+                        m0 = gl * WORDS + u * P
+                        nc.tensor.transpose(a_ps[:, gl, :, u], a_words[:, m0 : m0 + P], ident[:])
+                        for e in range(HARM):
+                            nc.tensor.transpose(y_ps[gl][:, :, 2 * u + e], y[:, e, m0 : m0 + P], ident[:])
+
+                sin_b = trig.tile([P, GROUP, K_PASS], F32)
+                abs_b = trig.tile([P, GROUP, K_PASS], F32)
+                for gl in range(GROUP):
+                    flat = y_ps[gl][:].rearrange("p d t -> p (d t)")
+                    nc.scalar.activation(out=sin_b[:, gl, :], in_=flat, func=ACT.Sin)
+                    nc.scalar.activation(out=abs_b[:, gl, :], in_=flat, func=ACT.Abs)
+                cos_b = trig.tile([P, GROUP, K_PASS], F32)
+                nc.scalar.activation(out=cos_b[:], in_=abs_b[:], func=ACT.Sin, scale=-1.0, bias=HALF_PI)
+
+                a_t = a_ps[:].rearrange("p g d u -> p (g d u)").bitcast(BF16)
+                asin_bf = trig.tile([P, GROUP * K_PASS], BF16, align_bytes=64)
+                nc.vector.tensor_tensor(
+                    out=asin_bf[:], in0=sin_b[:].rearrange("p g c -> p (g c)"), in1=a_t, op=ALU.mult
+                )
+                acos_bf = trig.tile([P, GROUP * K_PASS], BF16, align_bytes=64)
+                nc.vector.tensor_tensor(
+                    out=acos_bf[:], in0=cos_b[:].rearrange("p g c -> p (g c)"), in1=a_t, op=ALU.mult
+                )
+                for gl in range(GROUP):
+                    vals = slice(gl * K_PASS, (gl + 1) * K_PASS)
+                    nc.vector.quantize_mx(
+                        out=asin_codes[:, gl, d_rows].bitcast(FP8X4), scales=asin_scales[:, gl, d_rows], in_=asin_bf[:, vals]
+                    )
+                    nc.vector.quantize_mx(
+                        out=acos_codes[:, gl, d_rows].bitcast(FP8X4), scales=acos_scales[:, gl, d_rows], in_=acos_bf[:, vals]
+                    )
+
+            for gl in range(GROUP):
+                g = grp * GROUP + gl
+                r_cols = slice(g * P, (g + 1) * P)
+                nc.tensor.matmul_mx(
+                    out=acc[:],
+                    lhsT=sin_codes[:, r_cols].bitcast(FP8X4),
+                    lhsT_scale=sin_scales[:, r_cols],
+                    rhs=acos_codes[:, gl, :].bitcast(FP8X4),
+                    rhs_scale=acos_scales[:, gl, :],
+                    start=(g == 0),
+                    stop=False,
+                )
+                nc.tensor.matmul_mx(
+                    out=acc[:],
+                    lhsT=cos_codes[:, r_cols].bitcast(FP8X4),
+                    lhsT_scale=cos_scales[:, r_cols],
+                    rhs=asin_codes[:, gl, :].bitcast(FP8X4),
+                    rhs_scale=asin_scales[:, gl, :],
+                    start=False,
+                    stop=(g == PASSES - 1),
+                )
+
+        result = keep.tile([P, D_OUT], F32)
+        nc.vector.tensor_copy(out=result[:], in_=acc[:])
+        nc.sync.dma_start(out=out.flatten_outer_dims(), in_=result[:])

@@ -37,7 +37,7 @@ FLOPS = 2 * P * D_IN * Q + 2 * 2 * P * QK * D_OUT
 
 def reduce_angle(nc, pool, x, shape, name):
     turns = pool.tile([P] + shape, I32, name=name + "_turns")
-    nc.vector.tensor_scalar(out=turns[:], in0=x, scalar1=1.0 / TWO_PI, scalar2=None, op0=ALU.mult)
+    nc.gpsimd.tensor_scalar(out=turns[:], in0=x, scalar1=1.0 / TWO_PI, scalar2=0.0, op0=ALU.mult, op1=ALU.add)
     y = pool.tile([P] + shape, F32, name=name + "_y")
     nc.vector.scalar_tensor_tensor(
         out=y[:], in0=turns[:], scalar=-TWO_PI, in1=x, op0=ALU.mult, op1=ALU.add

@@ -1,4 +1,5 @@
 import math
+from contextlib import ExitStack
 
 import concourse.mybir as mybir
 from concourse.masks import make_identity
@@ -29,19 +30,25 @@ GROUP = 2
 GROUPS = PASSES // GROUP
 WORDS = K_PASS // HARM
 
+UNITS = GROUPS * D_BLOCKS
+
+FILL = 5
+
 TWO_PI = 2.0 * math.pi
 HALF_PI = 0.5 * math.pi
 
 FLOPS = 2 * P * D_IN * Q + 2 * 2 * P * QK * D_OUT
 
 
-def reduce_angle(nc, pool, x, shape, name):
-    turns = pool.tile([P] + shape, I32, name=name + "_turns")
-    nc.gpsimd.tensor_scalar(out=turns[:], in0=x, scalar1=1.0 / TWO_PI, scalar2=0.0, op0=ALU.mult, op1=ALU.add)
-    y = pool.tile([P] + shape, F32, name=name + "_y")
-    nc.vector.scalar_tensor_tensor(
-        out=y[:], in0=turns[:], scalar=-TWO_PI, in1=x, op0=ALU.mult, op1=ALU.add
-    )
+def whole_turns(engine, pool, x, shape, name):
+    turns = pool.tile([P] + shape, I32, name=name)
+    engine.tensor_scalar(out=turns[:], in0=x, scalar1=1.0 / TWO_PI, scalar2=0.0, op0=ALU.mult, op1=ALU.add)
+    return turns
+
+
+def subtract_turns(nc, pool, turns, x, shape, name):
+    y = pool.tile([P] + shape, F32, name=name)
+    nc.vector.scalar_tensor_tensor(out=y[:], in0=turns[:], scalar=-TWO_PI, in1=x, op0=ALU.mult, op1=ALU.add)
     return y
 
 
@@ -52,25 +59,26 @@ def tile_fourierkartlayer_k_kernel(tc, X0, t, Wc_w_words, Wc_w_scales, Wc_b, w, 
     a_rows = A.rearrange("d q k -> d (q k)")
     bp_rows = Bp.rearrange("d q k -> d (q k)")
 
-    with tc.tile_pool(name="keep", bufs=1) as keep, tc.tile_pool(name="wload", bufs=4) as wload, tc.tile_pool(
-        name="rows", bufs=2
-    ) as rows, tc.tile_pool(name="load", bufs=3) as load, tc.tile_pool(name="args", bufs=2) as args, tc.tile_pool(
-        name="trig", bufs=2
-    ) as trig, tc.tile_pool(name="codes", bufs=2) as codes, tc.psum_pool(name="ps_acc", bufs=1) as ps_acc, tc.psum_pool(
-        name="ps_a", bufs=2
-    ) as ps_a, tc.psum_pool(name="ps_y", bufs=4) as ps_y, tc.psum_pool(name="ps_c", bufs=1) as ps_c:
+    with ExitStack() as stack:
+        keep = stack.enter_context(tc.tile_pool(name="keep", bufs=1))
+        wload = stack.enter_context(tc.tile_pool(name="wload", bufs=4))
+        rows = stack.enter_context(tc.tile_pool(name="rows", bufs=2))
+        load = stack.enter_context(tc.tile_pool(name="load", bufs=6))
+        handoff = stack.enter_context(tc.tile_pool(name="handoff", bufs=1))
+        args = stack.enter_context(tc.tile_pool(name="args", bufs=2))
+        trig = stack.enter_context(tc.tile_pool(name="trig", bufs=2))
+        codes = stack.enter_context(tc.tile_pool(name="codes", bufs=2))
+        ps_acc = stack.enter_context(tc.psum_pool(name="ps_acc", bufs=1))
+        ps_a = stack.enter_context(tc.psum_pool(name="ps_a", bufs=2))
+        ps_y = stack.enter_context(tc.psum_pool(name="ps_y", bufs=4))
+        ps_c = stack.enter_context(tc.psum_pool(name="ps_c", bufs=1))
+        stack.enter_context(tc.manual_schedule())
+
         ident = keep.tile([P, P], F32)
         make_identity(nc, ident[:])
         ident_bf = keep.tile([P, P], BF16)
         make_identity(nc, ident_bf[:])
 
-        w_scales = keep.tile([P, Q], U8, align_bytes=64)
-        nc.vector.memset(w_scales[:].bitcast(I32), 0)
-        for quad in range(4):
-            nc.sync.dma_start(
-                out=w_scales[32 * quad : 32 * quad + 4, :].bitcast(I32),
-                in_=Wc_w_scales[0, 4 * quad : 4 * quad + 4, :].bitcast(I32),
-            )
         x0_sb = keep.tile([P, D_IN], BF16)
         nc.sync.dma_start(out=x0_sb[:], in_=x0_rows)
         bw_rows = keep.tile([P, P], BF16)
@@ -78,6 +86,13 @@ def tile_fourierkartlayer_k_kernel(tc, X0, t, Wc_w_words, Wc_w_scales, Wc_b, w, 
         nc.sync.dma_start(out=bw_rows[Q_BLOCKS:P, :], in_=w.rearrange("(j p) -> j p", p=P))
         t_bf = keep.tile([P, 2], BF16)
         nc.sync.dma_start(out=t_bf[:], in_=t.rearrange("b o -> (b o)").partition_broadcast(P))
+        w_scales = keep.tile([P, Q], U8, align_bytes=64)
+        nc.vector.memset(w_scales[:].bitcast(I32), 0)
+        for quad in range(4):
+            nc.sync.dma_start(
+                out=w_scales[32 * quad : 32 * quad + 4, :].bitcast(I32),
+                in_=Wc_w_scales[0, 4 * quad : 4 * quad + 4, :].bitcast(I32),
+            )
         t_f32 = keep.tile([P, 2], F32)
         nc.vector.tensor_copy(out=t_f32[:], in_=t_bf[:])
 
@@ -110,47 +125,57 @@ def tile_fourierkartlayer_k_kernel(tc, X0, t, Wc_w_words, Wc_w_scales, Wc_b, w, 
         sin_scales = keep.tile([P, PASSES * P], U8, align_bytes=64)
         cos_codes = keep.tile([P, PASSES * P], U32, align_bytes=64)
         cos_scales = keep.tile([P, PASSES * P], U8, align_bytes=64)
-        for grp in range(GROUPS):
-            first_block = grp * GROUP * 2
-            w_sb = wload.tile([P, GROUP * 2 * P], U32, align_bytes=64)
-            nc.sync.dma_start(
-                out=w_sb[:].bitcast(I32), in_=w_words[:, first_block * P : (first_block + GROUP * 2) * P]
-            )
-            c_ps = ps_c.tile([P, GROUP * 2, P], F32, tag="c")
+        width = GROUP * P * 2
+        live = {}
+
+        def load_w(grp):
+            w_sb = wload.tile([P, GROUP * 2 * P], U32, align_bytes=64, name="w_sb")
+            nc.sync.dma_start(out=w_sb[:].bitcast(I32), in_=w_words[:, grp * GROUP * 2 * P : (grp + 1) * GROUP * 2 * P])
+            live["w_sb", grp] = w_sb
+
+        def first_matmul(grp):
+            w_sb = live["w_sb", grp]
+            c_ps = ps_y.tile([P, GROUP * 2, P], F32, name="c_ps", tag="y_ps")
             for blk in range(GROUP * 2):
+                q_cols = slice((grp * GROUP * 2 + blk) * P, (grp * GROUP * 2 + blk + 1) * P)
                 nc.tensor.matmul_mx(
                     out=c_ps[:, blk, :],
                     lhsT=w_sb[:, blk * P : (blk + 1) * P].bitcast(FP8X4),
-                    lhsT_scale=w_scales[:, (first_block + blk) * P : (first_block + blk + 1) * P],
+                    lhsT_scale=w_scales[:, q_cols],
                     rhs=x0_codes[:].bitcast(FP8X4),
                     rhs_scale=x0_scales[:],
                     start=True,
                     stop=True,
                 )
-            k_angle = rows.tile([P, HARM, GROUP, P * 2], F32)
+            live["c_ps", grp] = c_ps
+
+        def row_angles(grp):
+            c_ps = live["c_ps", grp]
+            k_angle = rows.tile([P, HARM, GROUP, P * 2], F32, name="k_angle")
             for gl in range(GROUP):
-                blocks = slice(2 * gl, 2 * gl + 2)
+                blocks = slice(grp * GROUP * 2 + 2 * gl, grp * GROUP * 2 + 2 * gl + 2)
                 nc.vector.tensor_tensor(
                     out=k_angle[:, 0, gl, :].rearrange("p (b r u) -> p b r u", b=2, u=2),
-                    in0=c_ps[:, blocks, :].rearrange("p u (b r) -> p b r u", b=2),
-                    in1=shift[:, first_block + 2 * gl : first_block + 2 * gl + 2, :]
-                    .rearrange("p u b -> p b u")
-                    .unsqueeze(2)
-                    .to_broadcast([P, 2, S_LEN, 2]),
+                    in0=c_ps[:, 2 * gl : 2 * gl + 2, :].rearrange("p u (b r) -> p b r u", b=2),
+                    in1=shift[:, blocks, :].rearrange("p u b -> p b u").unsqueeze(2).to_broadcast([P, 2, S_LEN, 2]),
                     op=ALU.add,
                 )
             nc.vector.tensor_scalar(
                 out=k_angle[:, 1, :, :], in0=k_angle[:, 0, :, :], scalar1=2.0, scalar2=None, op0=ALU.mult
             )
-            width = GROUP * P * 2
-            y = reduce_angle(nc, rows, k_angle[:].rearrange("p e g c -> p e (g c)"), [HARM, width], "row")
-            y_abs = rows.tile([P, HARM, width], F32)
+            x = k_angle[:].rearrange("p e g c -> p e (g c)")
+            turns = whole_turns(nc.vector, rows, x, [HARM, width], "row_turns")
+            live["row_y", grp] = subtract_turns(nc, rows, turns, x, [HARM, width], "row_y")
+
+        def row_sines(grp):
+            y = live["row_y", grp]
+            y_abs = rows.tile([P, HARM, width], F32, name="row_abs")
             nc.scalar.activation(out=y_abs[:], in_=y[:], func=ACT.Abs)
-            sin_bf = rows.tile([P, width * HARM], BF16, align_bytes=64)
+            sin_bf = rows.tile([P, width * HARM], BF16, align_bytes=64, name="sin_bf")
             nc.scalar.activation(
                 out=sin_bf[:].rearrange("p (c e) -> p c e", e=HARM), in_=y[:].rearrange("p e c -> p c e"), func=ACT.Sin
             )
-            cos_bf = rows.tile([P, width * HARM], BF16, align_bytes=64)
+            cos_bf = rows.tile([P, width * HARM], BF16, align_bytes=64, name="cos_bf")
             nc.scalar.activation(
                 out=cos_bf[:].rearrange("p (c e) -> p c e", e=HARM),
                 in_=y_abs[:].rearrange("p e c -> p c e"),
@@ -158,66 +183,108 @@ def tile_fourierkartlayer_k_kernel(tc, X0, t, Wc_w_words, Wc_w_scales, Wc_b, w, 
                 scale=-1.0,
                 bias=HALF_PI,
             )
+            live["sin_bf", grp] = sin_bf
+            live["cos_bf", grp] = cos_bf
+
+        def quantise_rows(grp):
             cols = slice(grp * GROUP * P, (grp + 1) * GROUP * P)
+            sin_bf = live["sin_bf", grp]
+            cos_bf = live["cos_bf", grp]
             nc.vector.quantize_mx(out=sin_codes[:, cols].bitcast(FP8X4), scales=sin_scales[:, cols], in_=sin_bf[:])
             nc.vector.quantize_mx(out=cos_codes[:, cols].bitcast(FP8X4), scales=cos_scales[:, cols], in_=cos_bf[:])
 
+        def row_step(step):
+            if 0 <= step + 3 < GROUPS:
+                load_w(step + 3)
+            if 0 <= step + 2 < GROUPS:
+                first_matmul(step + 2)
+            if 0 <= step + 1 < GROUPS:
+                row_angles(step + 1)
+            if 0 <= step < GROUPS:
+                row_sines(step)
+            if 0 <= step - 1 < GROUPS:
+                quantise_rows(step - 1)
+
         acc = ps_acc.tile([P, D_OUT], F32)
-        for grp in range(GROUPS):
-            qk_cols = slice(grp * GROUP * K_PASS, (grp + 1) * GROUP * K_PASS)
-            acos_codes = codes.tile([P, GROUP, D_OUT], U32, align_bytes=64)
-            acos_scales = codes.tile([P, GROUP, D_OUT], U8, align_bytes=64)
-            asin_codes = codes.tile([P, GROUP, D_OUT], U32, align_bytes=64)
-            asin_scales = codes.tile([P, GROUP, D_OUT], U8, align_bytes=64)
-            for j in range(D_BLOCKS):
-                d_rows = slice(j * P, (j + 1) * P)
-                bp_sb = load.tile([P, GROUP * K_PASS], BF16)
-                nc.sync.dma_start(out=bp_sb[:], in_=bp_rows[d_rows, qk_cols])
-                a_sb = load.tile([P, GROUP * K_PASS], BF16)
-                nc.sync.dma_start(out=a_sb[:], in_=a_rows[d_rows, qk_cols])
 
-                y = reduce_angle(
-                    nc, args, bp_sb[:].rearrange("p (m e) -> p e m", e=HARM), [HARM, GROUP * WORDS], "phase"
-                )
+        def phases(k):
+            return live["bp_sb", k][:].rearrange("p (m e) -> p e m", e=HARM)
 
-                a_words = a_sb[:].bitcast(F32)
-                a_ps = ps_a.tile([P, GROUP, P, 2], F32)
-                y_ps = []
-                for gl in range(GROUP):
-                    y_ps.append(ps_y.tile([P, P, PACK], F32, name="y_ps"))
-                    for u in range(2):
+        def load_unit(k):
+            d_rows = slice((k % D_BLOCKS) * P, (k % D_BLOCKS + 1) * P)
+            qk_cols = slice((k // D_BLOCKS) * GROUP * K_PASS, (k // D_BLOCKS + 1) * GROUP * K_PASS)
+            bp_sb = load.tile([P, GROUP * K_PASS], BF16, name="bp_sb")
+            nc.sync.dma_start(out=bp_sb[:], in_=bp_rows[d_rows, qk_cols])
+            a_sb = load.tile([P, GROUP * K_PASS], BF16, name="a_sb")
+            nc.sync.dma_start(out=a_sb[:], in_=a_rows[d_rows, qk_cols])
+            live["bp_sb", k] = bp_sb
+            live["a_sb", k] = a_sb
+
+        def count_turns(k):
+            live["turns", k] = whole_turns(nc.gpsimd, handoff, phases(k), [HARM, GROUP * WORDS], "phase_turns")
+
+        def reduce_phases(k):
+            live["y", k] = subtract_turns(nc, args, live["turns", k], phases(k), [HARM, GROUP * WORDS], "phase_y")
+
+        def transpose_a(k):
+            a_words = live["a_sb", k][:].bitcast(F32)
+            a_ps = ps_a.tile([P, GROUP, P, 2], F32, name="a_ps")
+            for gl in range(GROUP):
+                for u in range(2):
+                    m0 = gl * WORDS + u * P
+                    nc.tensor.transpose(a_ps[:, gl, :, u], a_words[:, m0 : m0 + P], ident[:])
+            live["a_ps", k] = a_ps
+
+        def transpose_y(k):
+            y = live["y", k]
+            for gl in range(GROUP):
+                y_ps = ps_y.tile([P, P, PACK], F32, name="y_ps")
+                for u in range(2):
+                    for e in range(HARM):
                         m0 = gl * WORDS + u * P
-                        nc.tensor.transpose(a_ps[:, gl, :, u], a_words[:, m0 : m0 + P], ident[:])
-                        for e in range(HARM):
-                            nc.tensor.transpose(y_ps[gl][:, :, 2 * u + e], y[:, e, m0 : m0 + P], ident[:])
+                        nc.tensor.transpose(y_ps[:, :, 2 * u + e], y[:, e, m0 : m0 + P], ident[:])
+                live["y_ps", k, gl] = y_ps
 
-                sin_b = trig.tile([P, GROUP, K_PASS], F32)
-                abs_b = trig.tile([P, GROUP, K_PASS], F32)
-                for gl in range(GROUP):
-                    flat = y_ps[gl][:].rearrange("p d t -> p (d t)")
-                    nc.scalar.activation(out=sin_b[:, gl, :], in_=flat, func=ACT.Sin)
-                    nc.scalar.activation(out=abs_b[:, gl, :], in_=flat, func=ACT.Abs)
-                cos_b = trig.tile([P, GROUP, K_PASS], F32)
-                nc.scalar.activation(out=cos_b[:], in_=abs_b[:], func=ACT.Sin, scale=-1.0, bias=HALF_PI)
+        def phase_sines(k):
+            sin_cos = trig.tile([P, 2, GROUP, K_PASS], F32, name="sin_cos")
+            abs_b = trig.tile([P, GROUP, K_PASS], F32, name="abs_b")
+            for gl in range(GROUP):
+                flat = live["y_ps", k, gl][:].rearrange("p d t -> p (d t)")
+                nc.scalar.activation(out=sin_cos[:, 0, gl, :], in_=flat, func=ACT.Sin)
+                nc.scalar.activation(out=abs_b[:, gl, :], in_=flat, func=ACT.Abs)
+            nc.scalar.activation(out=sin_cos[:, 1, :, :], in_=abs_b[:], func=ACT.Sin, scale=-1.0, bias=HALF_PI)
+            live["sin_cos", k] = sin_cos
 
-                a_t = a_ps[:].rearrange("p g d u -> p (g d u)").bitcast(BF16)
-                asin_bf = trig.tile([P, GROUP * K_PASS], BF16, align_bytes=64)
-                nc.vector.tensor_tensor(
-                    out=asin_bf[:], in0=sin_b[:].rearrange("p g c -> p (g c)"), in1=a_t, op=ALU.mult
-                )
-                acos_bf = trig.tile([P, GROUP * K_PASS], BF16, align_bytes=64)
-                nc.vector.tensor_tensor(
-                    out=acos_bf[:], in0=cos_b[:].rearrange("p g c -> p (g c)"), in1=a_t, op=ALU.mult
-                )
-                for gl in range(GROUP):
-                    vals = slice(gl * K_PASS, (gl + 1) * K_PASS)
-                    nc.vector.quantize_mx(
-                        out=asin_codes[:, gl, d_rows].bitcast(FP8X4), scales=asin_scales[:, gl, d_rows], in_=asin_bf[:, vals]
+        def multiply(k):
+            a_t = live["a_ps", k][:].rearrange("p g d u -> p (g d u)").bitcast(BF16)
+            products = trig.tile([P, 2, GROUP * K_PASS], BF16, align_bytes=64, name="products")
+            nc.vector.tensor_tensor(
+                out=products[:],
+                in0=live["sin_cos", k][:].rearrange("p f g c -> p f (g c)"),
+                in1=a_t.unsqueeze(1).to_broadcast([P, 2, GROUP * K_PASS]),
+                op=ALU.mult,
+            )
+            live["products", k] = products
+
+        def quantise(k):
+            grp = k // D_BLOCKS
+            d_cols = slice((k % D_BLOCKS) * P, (k % D_BLOCKS + 1) * P)
+            for f, name in enumerate(("sin", "cos")):
+                if k % D_BLOCKS == 0:
+                    live["a" + name + "_codes", grp] = codes.tile(
+                        [P, GROUP, D_OUT], U32, align_bytes=64, name="a" + name + "_codes"
                     )
+                    live["a" + name + "_scales", grp] = codes.tile(
+                        [P, GROUP, D_OUT], U8, align_bytes=64, name="a" + name + "_scales"
+                    )
+                for gl in range(GROUP):
                     nc.vector.quantize_mx(
-                        out=acos_codes[:, gl, d_rows].bitcast(FP8X4), scales=acos_scales[:, gl, d_rows], in_=acos_bf[:, vals]
+                        out=live["a" + name + "_codes", grp][:, gl, d_cols].bitcast(FP8X4),
+                        scales=live["a" + name + "_scales", grp][:, gl, d_cols],
+                        in_=live["products", k][:, f, gl * K_PASS : (gl + 1) * K_PASS],
                     )
 
+        def long_sums(grp):
             for gl in range(GROUP):
                 g = grp * GROUP + gl
                 r_cols = slice(g * P, (g + 1) * P)
@@ -225,8 +292,8 @@ def tile_fourierkartlayer_k_kernel(tc, X0, t, Wc_w_words, Wc_w_scales, Wc_b, w, 
                     out=acc[:],
                     lhsT=sin_codes[:, r_cols].bitcast(FP8X4),
                     lhsT_scale=sin_scales[:, r_cols],
-                    rhs=acos_codes[:, gl, :].bitcast(FP8X4),
-                    rhs_scale=acos_scales[:, gl, :],
+                    rhs=live["acos_codes", grp][:, gl, :].bitcast(FP8X4),
+                    rhs_scale=live["acos_scales", grp][:, gl, :],
                     start=(g == 0),
                     stop=False,
                 )
@@ -234,11 +301,38 @@ def tile_fourierkartlayer_k_kernel(tc, X0, t, Wc_w_words, Wc_w_scales, Wc_b, w, 
                     out=acc[:],
                     lhsT=cos_codes[:, r_cols].bitcast(FP8X4),
                     lhsT_scale=cos_scales[:, r_cols],
-                    rhs=asin_codes[:, gl, :].bitcast(FP8X4),
-                    rhs_scale=asin_scales[:, gl, :],
+                    rhs=live["asin_codes", grp][:, gl, :].bitcast(FP8X4),
+                    rhs_scale=live["asin_scales", grp][:, gl, :],
                     start=False,
                     stop=(g == PASSES - 1),
                 )
+
+        def unit_step(step):
+            if 0 <= step + 5 < UNITS:
+                load_unit(step + 5)
+            if 0 <= step - 2 < UNITS and (step - 2) % D_BLOCKS == D_BLOCKS - 1:
+                long_sums((step - 2) // D_BLOCKS)
+            if 0 <= step + 2 < UNITS:
+                reduce_phases(step + 2)
+            if 0 <= step + 3 < UNITS:
+                count_turns(step + 3)
+            if 0 <= step + 1 < UNITS:
+                transpose_a(step + 1)
+            if 0 <= step + 2 < UNITS:
+                transpose_y(step + 2)
+            if 0 <= step + 1 < UNITS:
+                phase_sines(step + 1)
+            if 0 <= step < UNITS:
+                multiply(step)
+            if 0 <= step - 1 < UNITS:
+                quantise(step - 1)
+
+        for step in range(-3, GROUPS + 1):
+            row_step(step)
+            if step > GROUPS - FILL:
+                unit_step(step - GROUPS - 1)
+        for step in range(UNITS + 2):
+            unit_step(step)
 
         result = keep.tile([P, D_OUT], F32)
         nc.vector.tensor_copy(out=result[:], in_=acc[:])

@@ -28,11 +28,12 @@ PASSES = QK // K_PASS
 D_BLOCKS = D_OUT // P
 GROUP = 2
 GROUPS = PASSES // GROUP
+PAIR = 2
+UNITS_PER_PASS = D_BLOCKS // PAIR
 WORDS = K_PASS // HARM
 
-UNITS = GROUPS * D_BLOCKS
-
-FILL = 5
+UNITS = PASSES * UNITS_PER_PASS
+UNITS_PER_GROUP = GROUP * UNITS_PER_PASS
 
 TWO_PI = 2.0 * math.pi
 HALF_PI = 0.5 * math.pi
@@ -61,9 +62,9 @@ def tile_fourierkartlayer_k_kernel(tc, X0, t, Wc_w_words, Wc_w_scales, Wc_b, w, 
 
     with ExitStack() as stack:
         keep = stack.enter_context(tc.tile_pool(name="keep", bufs=1))
-        wload = stack.enter_context(tc.tile_pool(name="wload", bufs=4))
-        rows = stack.enter_context(tc.tile_pool(name="rows", bufs=2))
-        load = stack.enter_context(tc.tile_pool(name="load", bufs=6))
+        wload = stack.enter_context(tc.tile_pool(name="wload", bufs=2))
+        rows = stack.enter_context(tc.tile_pool(name="rows", bufs=1))
+        load = stack.enter_context(tc.tile_pool(name="load", bufs=7))
         handoff = stack.enter_context(tc.tile_pool(name="handoff", bufs=1))
         args = stack.enter_context(tc.tile_pool(name="args", bufs=2))
         trig = stack.enter_context(tc.tile_pool(name="trig", bufs=2))
@@ -135,7 +136,7 @@ def tile_fourierkartlayer_k_kernel(tc, X0, t, Wc_w_words, Wc_w_scales, Wc_b, w, 
 
         def first_matmul(grp):
             w_sb = live["w_sb", grp]
-            c_ps = ps_y.tile([P, GROUP * 2, P], F32, name="c_ps", tag="y_ps")
+            c_ps = ps_c.tile([P, GROUP * 2, P], F32, name="c_ps", tag="c")
             for blk in range(GROUP * 2):
                 q_cols = slice((grp * GROUP * 2 + blk) * P, (grp * GROUP * 2 + blk + 1) * P)
                 nc.tensor.matmul_mx(
@@ -160,10 +161,14 @@ def tile_fourierkartlayer_k_kernel(tc, X0, t, Wc_w_words, Wc_w_scales, Wc_b, w, 
                     in1=shift[:, blocks, :].rearrange("p u b -> p b u").unsqueeze(2).to_broadcast([P, 2, S_LEN, 2]),
                     op=ALU.add,
                 )
-            nc.vector.tensor_scalar(
-                out=k_angle[:, 1, :, :], in0=k_angle[:, 0, :, :], scalar1=2.0, scalar2=None, op0=ALU.mult
-            )
-            x = k_angle[:].rearrange("p e g c -> p e (g c)")
+            live["k_angle", grp] = k_angle
+
+        def row_double(grp):
+            k_angle = live["k_angle", grp]
+            nc.scalar.mul(out=k_angle[:, 1, :, :], in_=k_angle[:, 0, :, :], mul=2.0)
+
+        def row_reduce(grp):
+            x = live["k_angle", grp][:].rearrange("p e g c -> p e (g c)")
             turns = whole_turns(nc.vector, rows, x, [HARM, width], "row_turns")
             live["row_y", grp] = subtract_turns(nc, rows, turns, x, [HARM, width], "row_y")
 
@@ -193,146 +198,137 @@ def tile_fourierkartlayer_k_kernel(tc, X0, t, Wc_w_words, Wc_w_scales, Wc_b, w, 
             nc.vector.quantize_mx(out=sin_codes[:, cols].bitcast(FP8X4), scales=sin_scales[:, cols], in_=sin_bf[:])
             nc.vector.quantize_mx(out=cos_codes[:, cols].bitcast(FP8X4), scales=cos_scales[:, cols], in_=cos_bf[:])
 
-        def row_step(step):
-            if 0 <= step + 3 < GROUPS:
-                load_w(step + 3)
-            if 0 <= step + 2 < GROUPS:
-                first_matmul(step + 2)
-            if 0 <= step + 1 < GROUPS:
-                row_angles(step + 1)
-            if 0 <= step < GROUPS:
-                row_sines(step)
-            if 0 <= step - 1 < GROUPS:
-                quantise_rows(step - 1)
-
         acc = ps_acc.tile([P, D_OUT], F32)
 
         def phases(k):
-            return live["bp_sb", k][:].rearrange("p (m e) -> p e m", e=HARM)
+            return live["bp_sb", k][:].rearrange("p (n e) -> p e n", e=HARM)
 
         def load_unit(k):
-            d_rows = slice((k % D_BLOCKS) * P, (k % D_BLOCKS + 1) * P)
-            qk_cols = slice((k // D_BLOCKS) * GROUP * K_PASS, (k // D_BLOCKS + 1) * GROUP * K_PASS)
-            bp_sb = load.tile([P, GROUP * K_PASS], BF16, name="bp_sb")
-            nc.sync.dma_start(out=bp_sb[:], in_=bp_rows[d_rows, qk_cols])
-            a_sb = load.tile([P, GROUP * K_PASS], BF16, name="a_sb")
-            nc.sync.dma_start(out=a_sb[:], in_=a_rows[d_rows, qk_cols])
-            live["bp_sb", k] = bp_sb
-            live["a_sb", k] = a_sb
+            g, half = divmod(k, UNITS_PER_PASS)
+            d_rows = slice(half * PAIR * P, (half + 1) * PAIR * P)
+            qk_cols = slice(g * K_PASS, (g + 1) * K_PASS)
+            for name, source in (("bp_sb", bp_rows), ("a_sb", a_rows)):
+                sb = load.tile([P, PAIR * K_PASS], BF16, name=name)
+                nc.sync.dma_start(
+                    out=sb[:].rearrange("p (j c) -> p j c", j=PAIR),
+                    in_=source[d_rows, qk_cols].rearrange("(j p) c -> p j c", p=P),
+                )
+                live[name, k] = sb
 
         def count_turns(k):
-            live["turns", k] = whole_turns(nc.gpsimd, handoff, phases(k), [HARM, GROUP * WORDS], "phase_turns")
+            live["turns", k] = whole_turns(nc.gpsimd, handoff, phases(k), [HARM, PAIR * WORDS], "phase_turns")
 
         def reduce_phases(k):
-            live["y", k] = subtract_turns(nc, args, live["turns", k], phases(k), [HARM, GROUP * WORDS], "phase_y")
+            live["y", k] = subtract_turns(nc, args, live["turns", k], phases(k), [HARM, PAIR * WORDS], "phase_y")
 
         def transpose_a(k):
             a_words = live["a_sb", k][:].bitcast(F32)
-            a_ps = ps_a.tile([P, GROUP, P, 2], F32, name="a_ps")
-            for gl in range(GROUP):
+            a_ps = ps_a.tile([P, PAIR, P, 2], F32, name="a_ps")
+            for j in range(PAIR):
                 for u in range(2):
-                    m0 = gl * WORDS + u * P
-                    nc.tensor.transpose(a_ps[:, gl, :, u], a_words[:, m0 : m0 + P], ident[:])
+                    m0 = j * WORDS + u * P
+                    nc.tensor.transpose(a_ps[:, j, :, u], a_words[:, m0 : m0 + P], ident[:])
             live["a_ps", k] = a_ps
 
         def transpose_y(k):
             y = live["y", k]
-            for gl in range(GROUP):
+            for j in range(PAIR):
                 y_ps = ps_y.tile([P, P, PACK], F32, name="y_ps")
                 for u in range(2):
                     for e in range(HARM):
-                        m0 = gl * WORDS + u * P
+                        m0 = j * WORDS + u * P
                         nc.tensor.transpose(y_ps[:, :, 2 * u + e], y[:, e, m0 : m0 + P], ident[:])
-                live["y_ps", k, gl] = y_ps
+                live["y_ps", k, j] = y_ps
 
         def phase_sines(k):
-            sin_cos = trig.tile([P, 2, GROUP, K_PASS], F32, name="sin_cos")
-            abs_b = trig.tile([P, GROUP, K_PASS], F32, name="abs_b")
-            for gl in range(GROUP):
-                flat = live["y_ps", k, gl][:].rearrange("p d t -> p (d t)")
-                nc.scalar.activation(out=sin_cos[:, 0, gl, :], in_=flat, func=ACT.Sin)
-                nc.scalar.activation(out=abs_b[:, gl, :], in_=flat, func=ACT.Abs)
+            sin_cos = trig.tile([P, 2, PAIR, K_PASS], F32, name="sin_cos", bufs=3)
+            abs_b = trig.tile([P, PAIR, K_PASS], F32, name="abs_b")
+            for j in range(PAIR):
+                flat = live["y_ps", k, j][:].rearrange("p d t -> p (d t)")
+                nc.scalar.activation(out=sin_cos[:, 0, j, :], in_=flat, func=ACT.Sin)
+                nc.scalar.activation(out=abs_b[:, j, :], in_=flat, func=ACT.Abs)
             nc.scalar.activation(out=sin_cos[:, 1, :, :], in_=abs_b[:], func=ACT.Sin, scale=-1.0, bias=HALF_PI)
             live["sin_cos", k] = sin_cos
 
         def multiply(k):
-            a_t = live["a_ps", k][:].rearrange("p g d u -> p (g d u)").bitcast(BF16)
-            products = trig.tile([P, 2, GROUP * K_PASS], BF16, align_bytes=64, name="products")
+            a_t = live["a_ps", k][:].rearrange("p j d u -> p (j d u)").bitcast(BF16)
+            products = trig.tile([P, 2, PAIR * K_PASS], BF16, align_bytes=64, name="products")
             nc.vector.tensor_tensor(
                 out=products[:],
-                in0=live["sin_cos", k][:].rearrange("p f g c -> p f (g c)"),
-                in1=a_t.unsqueeze(1).to_broadcast([P, 2, GROUP * K_PASS]),
+                in0=live["sin_cos", k][:].rearrange("p f j c -> p f (j c)"),
+                in1=a_t.unsqueeze(1).to_broadcast([P, 2, PAIR * K_PASS]),
                 op=ALU.mult,
             )
             live["products", k] = products
 
         def quantise(k):
-            grp = k // D_BLOCKS
-            d_cols = slice((k % D_BLOCKS) * P, (k % D_BLOCKS + 1) * P)
-            for f, name in enumerate(("sin", "cos")):
-                if k % D_BLOCKS == 0:
-                    live["a" + name + "_codes", grp] = codes.tile(
-                        [P, GROUP, D_OUT], U32, align_bytes=64, name="a" + name + "_codes"
-                    )
-                    live["a" + name + "_scales", grp] = codes.tile(
-                        [P, GROUP, D_OUT], U8, align_bytes=64, name="a" + name + "_scales"
-                    )
-                for gl in range(GROUP):
-                    nc.vector.quantize_mx(
-                        out=live["a" + name + "_codes", grp][:, gl, d_cols].bitcast(FP8X4),
-                        scales=live["a" + name + "_scales", grp][:, gl, d_cols],
-                        in_=live["products", k][:, f, gl * K_PASS : (gl + 1) * K_PASS],
-                    )
-
-        def long_sums(grp):
-            for gl in range(GROUP):
-                g = grp * GROUP + gl
-                r_cols = slice(g * P, (g + 1) * P)
-                nc.tensor.matmul_mx(
-                    out=acc[:],
-                    lhsT=sin_codes[:, r_cols].bitcast(FP8X4),
-                    lhsT_scale=sin_scales[:, r_cols],
-                    rhs=live["acos_codes", grp][:, gl, :].bitcast(FP8X4),
-                    rhs_scale=live["acos_scales", grp][:, gl, :],
-                    start=(g == 0),
-                    stop=False,
-                )
-                nc.tensor.matmul_mx(
-                    out=acc[:],
-                    lhsT=cos_codes[:, r_cols].bitcast(FP8X4),
-                    lhsT_scale=cos_scales[:, r_cols],
-                    rhs=live["asin_codes", grp][:, gl, :].bitcast(FP8X4),
-                    rhs_scale=live["asin_scales", grp][:, gl, :],
-                    start=False,
-                    stop=(g == PASSES - 1),
+            g, half = divmod(k, UNITS_PER_PASS)
+            d_cols = slice(half * PAIR * P, (half + 1) * PAIR * P)
+            for f, name in enumerate(("asin", "acos")):
+                if half == 0:
+                    live[name + "_codes", g] = codes.tile([P, D_OUT], U32, align_bytes=64, name=name + "_codes")
+                    live[name + "_scales", g] = codes.tile([P, D_OUT], U8, align_bytes=64, name=name + "_scales")
+                nc.vector.quantize_mx(
+                    out=live[name + "_codes", g][:, d_cols].bitcast(FP8X4),
+                    scales=live[name + "_scales", g][:, d_cols],
+                    in_=live["products", k][:, f, :],
                 )
 
-        def unit_step(step):
-            if 0 <= step + 5 < UNITS:
-                load_unit(step + 5)
-            if 0 <= step - 2 < UNITS and (step - 2) % D_BLOCKS == D_BLOCKS - 1:
-                long_sums((step - 2) // D_BLOCKS)
-            if 0 <= step + 2 < UNITS:
-                reduce_phases(step + 2)
-            if 0 <= step + 3 < UNITS:
-                count_turns(step + 3)
+        def long_sums(g):
+            r_cols = slice(g * P, (g + 1) * P)
+            nc.tensor.matmul_mx(
+                out=acc[:],
+                lhsT=sin_codes[:, r_cols].bitcast(FP8X4),
+                lhsT_scale=sin_scales[:, r_cols],
+                rhs=live["acos_codes", g][:].bitcast(FP8X4),
+                rhs_scale=live["acos_scales", g][:],
+                start=(g == 0),
+                stop=False,
+            )
+            nc.tensor.matmul_mx(
+                out=acc[:],
+                lhsT=cos_codes[:, r_cols].bitcast(FP8X4),
+                lhsT_scale=cos_scales[:, r_cols],
+                rhs=live["asin_codes", g][:].bitcast(FP8X4),
+                rhs_scale=live["asin_scales", g][:],
+                start=False,
+                stop=(g == PASSES - 1),
+            )
+
+        for step in range(-2 * UNITS_PER_GROUP, UNITS + 2):
+            ahead, part = divmod(step + UNITS_PER_GROUP, UNITS_PER_GROUP)
+            if 0 <= step + 6 < UNITS:
+                load_unit(step + 6)
+            if part == 0 and 0 <= ahead + 1 < GROUPS:
+                load_w(ahead + 1)
+            if step >= 3 and (step - 3) % UNITS_PER_PASS == 0:
+                long_sums((step - 3) // UNITS_PER_PASS)
+            if part == 0 and 0 <= ahead < GROUPS:
+                first_matmul(ahead)
             if 0 <= step + 1 < UNITS:
                 transpose_a(step + 1)
+            if 0 <= step + 3 < UNITS:
+                reduce_phases(step + 3)
+            if 0 <= step + 4 < UNITS:
+                count_turns(step + 4)
+            if 0 <= step + 3 < UNITS:
+                transpose_y(step + 3)
             if 0 <= step + 2 < UNITS:
-                transpose_y(step + 2)
-            if 0 <= step + 1 < UNITS:
-                phase_sines(step + 1)
+                phase_sines(step + 2)
+            if part == 2 and 0 <= ahead < GROUPS:
+                row_double(ahead)
+            if part == 0 and 0 <= ahead - 1 < GROUPS:
+                row_sines(ahead - 1)
             if 0 <= step < UNITS:
                 multiply(step)
             if 0 <= step - 1 < UNITS:
                 quantise(step - 1)
-
-        for step in range(-3, GROUPS + 1):
-            row_step(step)
-            if step > GROUPS - FILL:
-                unit_step(step - GROUPS - 1)
-        for step in range(UNITS + 2):
-            unit_step(step)
+            if part == 1 and 0 <= ahead < GROUPS:
+                row_angles(ahead)
+            if part == 3 and 0 <= ahead < GROUPS:
+                row_reduce(ahead)
+            if part == 1 and 0 <= ahead - 1 < GROUPS:
+                quantise_rows(ahead - 1)
 
         result = keep.tile([P, D_OUT], F32)
         nc.vector.tensor_copy(out=result[:], in_=acc[:])

@@ -34,6 +34,7 @@ WORDS = K_PASS // HARM
 
 UNITS = PASSES * UNITS_PER_PASS
 UNITS_PER_GROUP = GROUP * UNITS_PER_PASS
+ROWS_LEAD = 6
 
 TWO_PI = 2.0 * math.pi
 HALF_PI = 0.5 * math.pi
@@ -165,21 +166,32 @@ def tile_fourierkartlayer_k_kernel(tc, X0, t, Wc_w_words, Wc_w_scales, Wc_b, w, 
 
         def row_double(grp):
             k_angle = live["k_angle", grp]
-            nc.scalar.mul(out=k_angle[:, 1, :, :], in_=k_angle[:, 0, :, :], mul=2.0)
+            nc.gpsimd.tensor_scalar(
+                out=k_angle[:, 1, :, :], in0=k_angle[:, 0, :, :], scalar1=2.0, scalar2=0.0, op0=ALU.mult, op1=ALU.add
+            )
+            x = k_angle[:].rearrange("p e g c -> p e (g c)")
+            live["row_turns", grp] = whole_turns(nc.gpsimd, rows, x, [HARM, width], "row_turns")
 
         def row_reduce(grp):
             x = live["k_angle", grp][:].rearrange("p e g c -> p e (g c)")
-            turns = whole_turns(nc.vector, rows, x, [HARM, width], "row_turns")
-            live["row_y", grp] = subtract_turns(nc, rows, turns, x, [HARM, width], "row_y")
+            live["row_y", grp] = subtract_turns(nc, rows, live["row_turns", grp], x, [HARM, width], "row_y")
 
-        def row_sines(grp):
+        def row_magnitudes(grp):
             y = live["row_y", grp]
             y_abs = rows.tile([P, HARM, width], F32, name="row_abs")
             nc.scalar.activation(out=y_abs[:], in_=y[:], func=ACT.Abs)
+            live["row_abs", grp] = y_abs
+
+        def row_sines(grp):
+            y = live["row_y", grp]
             sin_bf = rows.tile([P, width * HARM], BF16, align_bytes=64, name="sin_bf")
             nc.scalar.activation(
                 out=sin_bf[:].rearrange("p (c e) -> p c e", e=HARM), in_=y[:].rearrange("p e c -> p c e"), func=ACT.Sin
             )
+            live["sin_bf", grp] = sin_bf
+
+        def row_cosines(grp):
+            y_abs = live["row_abs", grp]
             cos_bf = rows.tile([P, width * HARM], BF16, align_bytes=64, name="cos_bf")
             nc.scalar.activation(
                 out=cos_bf[:].rearrange("p (c e) -> p c e", e=HARM),
@@ -188,7 +200,6 @@ def tile_fourierkartlayer_k_kernel(tc, X0, t, Wc_w_words, Wc_w_scales, Wc_b, w, 
                 scale=-1.0,
                 bias=HALF_PI,
             )
-            live["sin_bf", grp] = sin_bf
             live["cos_bf", grp] = cos_bf
 
         def quantise_rows(grp):
@@ -199,9 +210,6 @@ def tile_fourierkartlayer_k_kernel(tc, X0, t, Wc_w_words, Wc_w_scales, Wc_b, w, 
             nc.vector.quantize_mx(out=cos_codes[:, cols].bitcast(FP8X4), scales=cos_scales[:, cols], in_=cos_bf[:])
 
         acc = ps_acc.tile([P, D_OUT], F32)
-
-        def phases(k):
-            return live["bp_sb", k][:].rearrange("p (n e) -> p e n", e=HARM)
 
         def load_unit(k):
             g, half = divmod(k, UNITS_PER_PASS)
@@ -216,10 +224,16 @@ def tile_fourierkartlayer_k_kernel(tc, X0, t, Wc_w_words, Wc_w_scales, Wc_b, w, 
                 live[name, k] = sb
 
         def count_turns(k):
-            live["turns", k] = whole_turns(nc.gpsimd, handoff, phases(k), [HARM, PAIR * WORDS], "phase_turns")
+            phases = live["bp_sb", k][:]
+            live["turns", k] = whole_turns(nc.gpsimd, handoff, phases, [PAIR * K_PASS], "phase_turns")
+            phase_f32 = args.tile([P, PAIR * K_PASS], F32, name="phase_f32")
+            nc.gpsimd.tensor_scalar(out=phase_f32[:], in0=phases, scalar1=1.0, scalar2=0.0, op0=ALU.mult, op1=ALU.add)
+            live["phase_f32", k] = phase_f32
 
         def reduce_phases(k):
-            live["y", k] = subtract_turns(nc, args, live["turns", k], phases(k), [HARM, PAIR * WORDS], "phase_y")
+            minus = args.tile([P, PAIR * K_PASS], F32, name="minus")
+            nc.vector.tensor_scalar(out=minus[:], in0=live["turns", k][:], scalar1=-TWO_PI, scalar2=None, op0=ALU.mult)
+            live["minus", k] = minus
 
         def transpose_a(k):
             a_words = live["a_sb", k][:].bitcast(F32)
@@ -231,13 +245,21 @@ def tile_fourierkartlayer_k_kernel(tc, X0, t, Wc_w_words, Wc_w_scales, Wc_b, w, 
             live["a_ps", k] = a_ps
 
         def transpose_y(k):
-            y = live["y", k]
             for j in range(PAIR):
                 y_ps = ps_y.tile([P, P, PACK], F32, name="y_ps")
                 for u in range(2):
                     for e in range(HARM):
-                        m0 = j * WORDS + u * P
-                        nc.tensor.transpose(y_ps[:, :, 2 * u + e], y[:, e, m0 : m0 + P], ident[:])
+                        c0 = j * K_PASS + u * 2 * P + e
+                        parts = (live["phase_f32", k], live["minus", k])
+                        for i, part in enumerate(parts):
+                            nc.tensor.matmul(
+                                out=y_ps[:, :, 2 * u + e],
+                                lhsT=part[:, c0 : c0 + 2 * P - e : 2],
+                                rhs=ident[:],
+                                is_transpose=True,
+                                start=(i == 0),
+                                stop=(i == len(parts) - 1),
+                            )
                 live["y_ps", k, j] = y_ps
 
         def phase_sines(k):
@@ -247,8 +269,13 @@ def tile_fourierkartlayer_k_kernel(tc, X0, t, Wc_w_words, Wc_w_scales, Wc_b, w, 
                 flat = live["y_ps", k, j][:].rearrange("p d t -> p (d t)")
                 nc.scalar.activation(out=sin_cos[:, 0, j, :], in_=flat, func=ACT.Sin)
                 nc.scalar.activation(out=abs_b[:, j, :], in_=flat, func=ACT.Abs)
-            nc.scalar.activation(out=sin_cos[:, 1, :, :], in_=abs_b[:], func=ACT.Sin, scale=-1.0, bias=HALF_PI)
             live["sin_cos", k] = sin_cos
+            live["abs_b", k] = abs_b
+
+        def phase_cosines(k):
+            nc.scalar.activation(
+                out=live["sin_cos", k][:, 1, :, :], in_=live["abs_b", k][:], func=ACT.Sin, scale=-1.0, bias=HALF_PI
+            )
 
         def multiply(k):
             a_t = live["a_ps", k][:].rearrange("p j d u -> p (j d u)").bitcast(BF16)
@@ -295,8 +322,8 @@ def tile_fourierkartlayer_k_kernel(tc, X0, t, Wc_w_words, Wc_w_scales, Wc_b, w, 
                 stop=(g == PASSES - 1),
             )
 
-        for step in range(-2 * UNITS_PER_GROUP, UNITS + 2):
-            ahead, part = divmod(step + UNITS_PER_GROUP, UNITS_PER_GROUP)
+        for step in range(-UNITS_PER_GROUP - ROWS_LEAD, UNITS + 2):
+            ahead, part = divmod(step + ROWS_LEAD, UNITS_PER_GROUP)
             if 0 <= step + 6 < UNITS:
                 load_unit(step + 6)
             if part == 0 and 0 <= ahead + 1 < GROUPS:
@@ -313,12 +340,18 @@ def tile_fourierkartlayer_k_kernel(tc, X0, t, Wc_w_words, Wc_w_scales, Wc_b, w, 
                 count_turns(step + 4)
             if 0 <= step + 3 < UNITS:
                 transpose_y(step + 3)
-            if 0 <= step + 2 < UNITS:
-                phase_sines(step + 2)
             if part == 2 and 0 <= ahead < GROUPS:
                 row_double(ahead)
+            if 0 <= step + 2 < UNITS:
+                phase_sines(step + 2)
+            if 0 <= step + 1 < UNITS:
+                phase_cosines(step + 1)
             if part == 0 and 0 <= ahead - 1 < GROUPS:
+                row_magnitudes(ahead - 1)
+            if part == 1 and 0 <= ahead - 1 < GROUPS:
                 row_sines(ahead - 1)
+            if part == 2 and 0 <= ahead - 1 < GROUPS:
+                row_cosines(ahead - 1)
             if 0 <= step < UNITS:
                 multiply(step)
             if 0 <= step - 1 < UNITS:
@@ -327,7 +360,7 @@ def tile_fourierkartlayer_k_kernel(tc, X0, t, Wc_w_words, Wc_w_scales, Wc_b, w, 
                 row_angles(ahead)
             if part == 3 and 0 <= ahead < GROUPS:
                 row_reduce(ahead)
-            if part == 1 and 0 <= ahead - 1 < GROUPS:
+            if part == 3 and 0 <= ahead - 1 < GROUPS:
                 quantise_rows(ahead - 1)
 
         result = keep.tile([P, D_OUT], F32)

@@ -246,14 +246,14 @@ def tile_fourierkartlayer_k_kernel(tc, X0, t, Wc_w_words, Wc_w_scales, Wc_b, w, 
 
         def transpose_y(k):
             for j in range(PAIR):
-                y_ps = ps_y.tile([P, P, PACK], F32, name="y_ps")
+                y_ps = ps_y.tile([P, PACK, P], F32, name="y_ps")
                 for u in range(2):
                     for e in range(HARM):
                         c0 = j * K_PASS + u * 2 * P + e
                         parts = (live["phase_f32", k], live["minus", k])
                         for i, part in enumerate(parts):
                             nc.tensor.matmul(
-                                out=y_ps[:, :, 2 * u + e],
+                                out=y_ps[:, 2 * u + e, :],
                                 lhsT=part[:, c0 : c0 + 2 * P - e : 2],
                                 rhs=ident[:],
                                 is_transpose=True,
@@ -266,9 +266,9 @@ def tile_fourierkartlayer_k_kernel(tc, X0, t, Wc_w_words, Wc_w_scales, Wc_b, w, 
             sin_cos = trig.tile([P, 2, PAIR, K_PASS], F32, name="sin_cos", bufs=3)
             abs_b = trig.tile([P, PAIR, K_PASS], F32, name="abs_b")
             for j in range(PAIR):
-                flat = live["y_ps", k, j][:].rearrange("p d t -> p (d t)")
-                nc.scalar.activation(out=sin_cos[:, 0, j, :], in_=flat, func=ACT.Sin)
-                nc.scalar.activation(out=abs_b[:, j, :], in_=flat, func=ACT.Abs)
+                y_t = live["y_ps", k, j][:].rearrange("p t d -> p d t")
+                nc.scalar.activation(out=sin_cos[:, 0, j, :].rearrange("p (d t) -> p d t", t=PACK), in_=y_t, func=ACT.Sin)
+                nc.scalar.activation(out=abs_b[:, j, :].rearrange("p (d t) -> p d t", t=PACK), in_=y_t, func=ACT.Abs)
             live["sin_cos", k] = sin_cos
             live["abs_b", k] = abs_b
 

@@ -32,9 +32,13 @@ PAIR = 2
 UNITS_PER_PASS = D_BLOCKS // PAIR
 WORDS = K_PASS // HARM
 
+QUARTER = PAIR * K_PASS // 4
+PLAIN_END = QUARTER
+WIDE_END = 3 * QUARTER
+
 UNITS = PASSES * UNITS_PER_PASS
 UNITS_PER_GROUP = GROUP * UNITS_PER_PASS
-ROWS_LEAD = 6
+ROWS_LEAD = 7
 
 TWO_PI = 2.0 * math.pi
 HALF_PI = 0.5 * math.pi
@@ -42,16 +46,12 @@ HALF_PI = 0.5 * math.pi
 FLOPS = 2 * P * D_IN * Q + 2 * 2 * P * QK * D_OUT
 
 
-def whole_turns(engine, pool, x, shape, name):
-    turns = pool.tile([P] + shape, I32, name=name)
-    engine.tensor_scalar(out=turns[:], in0=x, scalar1=1.0 / TWO_PI, scalar2=0.0, op0=ALU.mult, op1=ALU.add)
-    return turns
+def whole_turns(nc, turns, x, factor=1.0):
+    nc.gpsimd.tensor_scalar(out=turns, in0=x, scalar1=factor / TWO_PI, scalar2=0.0, op0=ALU.mult, op1=ALU.add)
 
 
-def subtract_turns(nc, pool, turns, x, shape, name):
-    y = pool.tile([P] + shape, F32, name=name)
-    nc.vector.scalar_tensor_tensor(out=y[:], in0=turns[:], scalar=-TWO_PI, in1=x, op0=ALU.mult, op1=ALU.add)
-    return y
+def subtract_turns(nc, y, turns, x):
+    nc.vector.scalar_tensor_tensor(out=y, in0=turns, scalar=-TWO_PI, in1=x, op0=ALU.mult, op1=ALU.add)
 
 
 def tile_fourierkartlayer_k_kernel(tc, X0, t, Wc_w_words, Wc_w_scales, Wc_b, w, A, Bp, out):
@@ -153,7 +153,7 @@ def tile_fourierkartlayer_k_kernel(tc, X0, t, Wc_w_words, Wc_w_scales, Wc_b, w, 
 
         def row_angles(grp):
             c_ps = live["c_ps", grp]
-            k_angle = rows.tile([P, HARM, GROUP, P * 2], F32, name="k_angle")
+            k_angle = rows.tile([P, HARM, GROUP, P * 2], F32, name="k_angle", bufs=2)
             for gl in range(GROUP):
                 blocks = slice(grp * GROUP * 2 + 2 * gl, grp * GROUP * 2 + 2 * gl + 2)
                 nc.vector.tensor_tensor(
@@ -169,12 +169,18 @@ def tile_fourierkartlayer_k_kernel(tc, X0, t, Wc_w_words, Wc_w_scales, Wc_b, w, 
             nc.gpsimd.tensor_scalar(
                 out=k_angle[:, 1, :, :], in0=k_angle[:, 0, :, :], scalar1=2.0, scalar2=0.0, op0=ALU.mult, op1=ALU.add
             )
-            x = k_angle[:].rearrange("p e g c -> p e (g c)")
-            live["row_turns", grp] = whole_turns(nc.gpsimd, rows, x, [HARM, width], "row_turns")
+
+        def row_turns(grp, e):
+            if e == 0:
+                live["row_turns", grp] = rows.tile([P, HARM, width], I32, name="row_turns", bufs=2)
+            angle = live["k_angle", grp][:, 0, :, :].rearrange("p g c -> p (g c)")
+            whole_turns(nc, live["row_turns", grp][:, e, :], angle, e + 1.0)
 
         def row_reduce(grp):
+            y = rows.tile([P, HARM, width], F32, name="row_y")
             x = live["k_angle", grp][:].rearrange("p e g c -> p e (g c)")
-            live["row_y", grp] = subtract_turns(nc, rows, live["row_turns", grp], x, [HARM, width], "row_y")
+            subtract_turns(nc, y[:], live["row_turns", grp][:], x)
+            live["row_y", grp] = y
 
         def row_magnitudes(grp):
             y = live["row_y", grp]
@@ -225,15 +231,23 @@ def tile_fourierkartlayer_k_kernel(tc, X0, t, Wc_w_words, Wc_w_scales, Wc_b, w, 
 
         def count_turns(k):
             phases = live["bp_sb", k][:]
-            live["turns", k] = whole_turns(nc.gpsimd, handoff, phases, [PAIR * K_PASS], "phase_turns")
-            phase_f32 = args.tile([P, PAIR * K_PASS], F32, name="phase_f32")
-            nc.gpsimd.tensor_scalar(out=phase_f32[:], in0=phases, scalar1=1.0, scalar2=0.0, op0=ALU.mult, op1=ALU.add)
-            live["phase_f32", k] = phase_f32
+            turns = handoff.tile([P, PAIR * K_PASS], I32, name="phase_turns")
+            whole_turns(nc, turns[:], phases)
+            live["turns", k] = turns
+            wide = args.tile([P, WIDE_END - PLAIN_END], F32, name="wide")
+            nc.gpsimd.tensor_scalar(
+                out=wide[:], in0=phases[:, PLAIN_END:WIDE_END], scalar1=1.0, scalar2=0.0, op0=ALU.mult, op1=ALU.add
+            )
+            live["wide", k] = wide
 
         def reduce_phases(k):
-            minus = args.tile([P, PAIR * K_PASS], F32, name="minus")
-            nc.vector.tensor_scalar(out=minus[:], in0=live["turns", k][:], scalar1=-TWO_PI, scalar2=None, op0=ALU.mult)
-            live["minus", k] = minus
+            turns = live["turns", k]
+            reduced = args.tile([P, PAIR * K_PASS], F32, name="reduced")
+            nc.vector.tensor_scalar(
+                out=reduced[:, :WIDE_END], in0=turns[:, :WIDE_END], scalar1=-TWO_PI, scalar2=None, op0=ALU.mult
+            )
+            subtract_turns(nc, reduced[:, WIDE_END:], turns[:, WIDE_END:], live["bp_sb", k][:, WIDE_END:])
+            live["reduced", k] = reduced
 
         def transpose_a(k):
             a_words = live["a_sb", k][:].bitcast(F32)
@@ -244,22 +258,39 @@ def tile_fourierkartlayer_k_kernel(tc, X0, t, Wc_w_words, Wc_w_scales, Wc_b, w, 
                     nc.tensor.transpose(a_ps[:, j, :, u], a_words[:, m0 : m0 + P], ident[:])
             live["a_ps", k] = a_ps
 
+        def every_second(tile, c0):
+            return tile[:, c0 : c0 + 2 * P - 1 : 2]
+
         def transpose_y(k):
             for j in range(PAIR):
                 y_ps = ps_y.tile([P, PACK, P], F32, name="y_ps")
                 for u in range(2):
                     for e in range(HARM):
                         c0 = j * K_PASS + u * 2 * P + e
-                        parts = (live["phase_f32", k], live["minus", k])
-                        for i, part in enumerate(parts):
+                        y_block = y_ps[:, 2 * u + e, :]
+                        alone = c0 >= WIDE_END
+                        if c0 < PLAIN_END:
+                            bp_sb = live["bp_sb", k]
                             nc.tensor.matmul(
-                                out=y_ps[:, 2 * u + e, :],
-                                lhsT=part[:, c0 : c0 + 2 * P - e : 2],
+                                out=y_block, lhsT=every_second(bp_sb, c0), rhs=ident_bf[:], start=True, stop=False
+                            )
+                        elif not alone:
+                            nc.tensor.matmul(
+                                out=y_block,
+                                lhsT=every_second(live["wide", k], c0 - PLAIN_END),
                                 rhs=ident[:],
                                 is_transpose=True,
-                                start=(i == 0),
-                                stop=(i == len(parts) - 1),
+                                start=True,
+                                stop=False,
                             )
+                        nc.tensor.matmul(
+                            out=y_block,
+                            lhsT=every_second(live["reduced", k], c0),
+                            rhs=ident[:],
+                            is_transpose=True,
+                            start=alone,
+                            stop=True,
+                        )
                 live["y_ps", k, j] = y_ps
 
         def phase_sines(k):
@@ -341,27 +372,31 @@ def tile_fourierkartlayer_k_kernel(tc, X0, t, Wc_w_words, Wc_w_scales, Wc_b, w, 
             if 0 <= step + 3 < UNITS:
                 transpose_y(step + 3)
             if part == 2 and 0 <= ahead < GROUPS:
+                row_turns(ahead, 0)
+            if part == 3 and 0 <= ahead < GROUPS:
                 row_double(ahead)
+            if part == 0 and 0 <= ahead - 1 < GROUPS:
+                row_turns(ahead - 1, 1)
             if 0 <= step + 2 < UNITS:
                 phase_sines(step + 2)
             if 0 <= step + 1 < UNITS:
                 phase_cosines(step + 1)
-            if part == 0 and 0 <= ahead - 1 < GROUPS:
-                row_magnitudes(ahead - 1)
-            if part == 1 and 0 <= ahead - 1 < GROUPS:
-                row_sines(ahead - 1)
             if part == 2 and 0 <= ahead - 1 < GROUPS:
-                row_cosines(ahead - 1)
+                row_magnitudes(ahead - 1)
+            if part == 3 and 0 <= ahead - 1 < GROUPS:
+                row_sines(ahead - 1)
+            if part == 0 and 0 <= ahead - 2 < GROUPS:
+                row_cosines(ahead - 2)
             if 0 <= step < UNITS:
                 multiply(step)
             if 0 <= step - 1 < UNITS:
                 quantise(step - 1)
             if part == 1 and 0 <= ahead < GROUPS:
                 row_angles(ahead)
-            if part == 3 and 0 <= ahead < GROUPS:
-                row_reduce(ahead)
-            if part == 3 and 0 <= ahead - 1 < GROUPS:
-                quantise_rows(ahead - 1)
+            if part == 1 and 0 <= ahead - 1 < GROUPS:
+                row_reduce(ahead - 1)
+            if part == 1 and 0 <= ahead - 2 < GROUPS:
+                quantise_rows(ahead - 2)
 
         result = keep.tile([P, D_OUT], F32)
         nc.vector.tensor_copy(out=result[:], in_=acc[:])

@@ -34,11 +34,11 @@ WORDS = K_PASS // HARM
 
 QUARTER = PAIR * K_PASS // 4
 PLAIN_END = QUARTER
-WIDE_END = 3 * QUARTER
+WIDE_END = 2 * QUARTER
 
 UNITS = PASSES * UNITS_PER_PASS
 UNITS_PER_GROUP = GROUP * UNITS_PER_PASS
-ROWS_LEAD = 7
+ROWS_LEAD = 8
 
 TWO_PI = 2.0 * math.pi
 HALF_PI = 0.5 * math.pi
@@ -46,12 +46,8 @@ HALF_PI = 0.5 * math.pi
 FLOPS = 2 * P * D_IN * Q + 2 * 2 * P * QK * D_OUT
 
 
-def whole_turns(nc, turns, x, factor=1.0):
-    nc.gpsimd.tensor_scalar(out=turns, in0=x, scalar1=factor / TWO_PI, scalar2=0.0, op0=ALU.mult, op1=ALU.add)
-
-
-def subtract_turns(nc, y, turns, x):
-    nc.vector.scalar_tensor_tensor(out=y, in0=turns, scalar=-TWO_PI, in1=x, op0=ALU.mult, op1=ALU.add)
+def whole_turns(nc, turns, x, factor):
+    nc.gpsimd.tensor_scalar(out=turns, in0=x, scalar1=factor, scalar2=0.0, op0=ALU.mult, op1=ALU.add)
 
 
 def tile_fourierkartlayer_k_kernel(tc, X0, t, Wc_w_words, Wc_w_scales, Wc_b, w, A, Bp, out):
@@ -153,34 +149,34 @@ def tile_fourierkartlayer_k_kernel(tc, X0, t, Wc_w_words, Wc_w_scales, Wc_b, w, 
 
         def row_angles(grp):
             c_ps = live["c_ps", grp]
-            k_angle = rows.tile([P, HARM, GROUP, P * 2], F32, name="k_angle", bufs=2)
+            angle = rows.tile([P, GROUP, P * 2], F32, name="angle", bufs=2)
             for gl in range(GROUP):
                 blocks = slice(grp * GROUP * 2 + 2 * gl, grp * GROUP * 2 + 2 * gl + 2)
                 nc.vector.tensor_tensor(
-                    out=k_angle[:, 0, gl, :].rearrange("p (b r u) -> p b r u", b=2, u=2),
+                    out=angle[:, gl, :].rearrange("p (b r u) -> p b r u", b=2, u=2),
                     in0=c_ps[:, 2 * gl : 2 * gl + 2, :].rearrange("p u (b r) -> p b r u", b=2),
                     in1=shift[:, blocks, :].rearrange("p u b -> p b u").unsqueeze(2).to_broadcast([P, 2, S_LEN, 2]),
                     op=ALU.add,
                 )
-            live["k_angle", grp] = k_angle
+            live["angle", grp] = angle
 
-        def row_double(grp):
-            k_angle = live["k_angle", grp]
-            nc.gpsimd.tensor_scalar(
-                out=k_angle[:, 1, :, :], in0=k_angle[:, 0, :, :], scalar1=2.0, scalar2=0.0, op0=ALU.mult, op1=ALU.add
-            )
+        def row_turns(grp, piece):
+            e, gl = divmod(piece, GROUP)
+            if piece == 0:
+                live["row_turns", grp] = rows.tile([P, HARM, GROUP, P * 2], I32, name="row_turns", bufs=2)
+            whole_turns(nc, live["row_turns", grp][:, e, gl, :], live["angle", grp][:, gl, :], (e + 1) / TWO_PI)
 
-        def row_turns(grp, e):
+        def row_reduce(grp, e):
             if e == 0:
-                live["row_turns", grp] = rows.tile([P, HARM, width], I32, name="row_turns", bufs=2)
-            angle = live["k_angle", grp][:, 0, :, :].rearrange("p g c -> p (g c)")
-            whole_turns(nc, live["row_turns", grp][:, e, :], angle, e + 1.0)
-
-        def row_reduce(grp):
-            y = rows.tile([P, HARM, width], F32, name="row_y")
-            x = live["k_angle", grp][:].rearrange("p e g c -> p e (g c)")
-            subtract_turns(nc, y[:], live["row_turns", grp][:], x)
-            live["row_y", grp] = y
+                live["row_y", grp] = rows.tile([P, HARM, width], F32, name="row_y")
+            nc.vector.scalar_tensor_tensor(
+                out=live["row_y", grp][:, e, :],
+                in0=live["angle", grp][:].rearrange("p g c -> p (g c)"),
+                scalar=(e + 1) / TWO_PI,
+                in1=live["row_turns", grp][:, e, :, :].rearrange("p g c -> p (g c)"),
+                op0=ALU.mult,
+                op1=ALU.subtract,
+            )
 
         def row_magnitudes(grp):
             y = live["row_y", grp]
@@ -192,7 +188,10 @@ def tile_fourierkartlayer_k_kernel(tc, X0, t, Wc_w_words, Wc_w_scales, Wc_b, w, 
             y = live["row_y", grp]
             sin_bf = rows.tile([P, width * HARM], BF16, align_bytes=64, name="sin_bf")
             nc.scalar.activation(
-                out=sin_bf[:].rearrange("p (c e) -> p c e", e=HARM), in_=y[:].rearrange("p e c -> p c e"), func=ACT.Sin
+                out=sin_bf[:].rearrange("p (c e) -> p c e", e=HARM),
+                in_=y[:].rearrange("p e c -> p c e"),
+                func=ACT.Sin,
+                scale=TWO_PI,
             )
             live["sin_bf", grp] = sin_bf
 
@@ -203,7 +202,7 @@ def tile_fourierkartlayer_k_kernel(tc, X0, t, Wc_w_words, Wc_w_scales, Wc_b, w, 
                 out=cos_bf[:].rearrange("p (c e) -> p c e", e=HARM),
                 in_=y_abs[:].rearrange("p e c -> p c e"),
                 func=ACT.Sin,
-                scale=-1.0,
+                scale=-TWO_PI,
                 bias=HALF_PI,
             )
             live["cos_bf", grp] = cos_bf
@@ -232,7 +231,7 @@ def tile_fourierkartlayer_k_kernel(tc, X0, t, Wc_w_words, Wc_w_scales, Wc_b, w, 
         def count_turns(k):
             phases = live["bp_sb", k][:]
             turns = handoff.tile([P, PAIR * K_PASS], I32, name="phase_turns")
-            whole_turns(nc, turns[:], phases)
+            whole_turns(nc, turns[:], phases, 1.0 / TWO_PI)
             live["turns", k] = turns
             wide = args.tile([P, WIDE_END - PLAIN_END], F32, name="wide")
             nc.gpsimd.tensor_scalar(
@@ -246,7 +245,14 @@ def tile_fourierkartlayer_k_kernel(tc, X0, t, Wc_w_words, Wc_w_scales, Wc_b, w, 
             nc.vector.tensor_scalar(
                 out=reduced[:, :WIDE_END], in0=turns[:, :WIDE_END], scalar1=-TWO_PI, scalar2=None, op0=ALU.mult
             )
-            subtract_turns(nc, reduced[:, WIDE_END:], turns[:, WIDE_END:], live["bp_sb", k][:, WIDE_END:])
+            nc.vector.scalar_tensor_tensor(
+                out=reduced[:, WIDE_END:],
+                in0=turns[:, WIDE_END:],
+                scalar=-TWO_PI,
+                in1=live["bp_sb", k][:, WIDE_END:],
+                op0=ALU.mult,
+                op1=ALU.add,
+            )
             live["reduced", k] = reduced
 
         def transpose_a(k):
@@ -371,31 +377,30 @@ def tile_fourierkartlayer_k_kernel(tc, X0, t, Wc_w_words, Wc_w_scales, Wc_b, w, 
                 count_turns(step + 4)
             if 0 <= step + 3 < UNITS:
                 transpose_y(step + 3)
-            if part == 2 and 0 <= ahead < GROUPS:
-                row_turns(ahead, 0)
-            if part == 3 and 0 <= ahead < GROUPS:
-                row_double(ahead)
-            if part == 0 and 0 <= ahead - 1 < GROUPS:
-                row_turns(ahead - 1, 1)
+            piece_group, piece = divmod(step + ROWS_LEAD - 2, UNITS_PER_GROUP)
+            if 0 <= piece_group < GROUPS:
+                row_turns(piece_group, piece)
             if 0 <= step + 2 < UNITS:
                 phase_sines(step + 2)
             if 0 <= step + 1 < UNITS:
                 phase_cosines(step + 1)
-            if part == 2 and 0 <= ahead - 1 < GROUPS:
-                row_magnitudes(ahead - 1)
             if part == 3 and 0 <= ahead - 1 < GROUPS:
-                row_sines(ahead - 1)
+                row_magnitudes(ahead - 1)
             if part == 0 and 0 <= ahead - 2 < GROUPS:
+                row_sines(ahead - 2)
+            if part == 1 and 0 <= ahead - 2 < GROUPS:
                 row_cosines(ahead - 2)
             if 0 <= step < UNITS:
                 multiply(step)
-            if 0 <= step - 1 < UNITS:
-                quantise(step - 1)
             if part == 1 and 0 <= ahead < GROUPS:
                 row_angles(ahead)
+            if 0 <= step - 1 < UNITS:
+                quantise(step - 1)
             if part == 1 and 0 <= ahead - 1 < GROUPS:
-                row_reduce(ahead - 1)
-            if part == 1 and 0 <= ahead - 2 < GROUPS:
+                row_reduce(ahead - 1, 0)
+            if part == 2 and 0 <= ahead - 1 < GROUPS:
+                row_reduce(ahead - 1, 1)
+            if part == 2 and 0 <= ahead - 2 < GROUPS:
                 quantise_rows(ahead - 2)
 
         result = keep.tile([P, D_OUT], F32)

@@ -38,6 +38,8 @@ WIDE_END = 2 * QUARTER
 
 UNITS = PASSES * UNITS_PER_PASS
 UNITS_PER_GROUP = GROUP * UNITS_PER_PASS
+EARLY = 2
+HEAD = 4
 ROWS_LEAD = 8
 
 TWO_PI = 2.0 * math.pi
@@ -77,6 +79,20 @@ def tile_fourierkartlayer_k_kernel(tc, X0, t, Wc_w_words, Wc_w_scales, Wc_b, w, 
         ident_bf = keep.tile([P, P], BF16)
         make_identity(nc, ident_bf[:])
 
+        live = {}
+
+        def load_rows(name, source, k):
+            g, half = divmod(k, UNITS_PER_PASS)
+            d_rows = slice(half * PAIR * P, (half + 1) * PAIR * P)
+            qk_cols = slice(g * K_PASS, (g + 1) * K_PASS)
+            sb = load.tile([P, PAIR * K_PASS], BF16, name=name)
+            nc.sync.dma_start(
+                out=sb[:].rearrange("p (j c) -> p j c", j=PAIR),
+                in_=source[d_rows, qk_cols].rearrange("(j p) c -> p j c", p=P),
+            )
+            live[name, k] = sb
+
+        load_rows("bp_sb", bp_rows, 0)
         x0_sb = keep.tile([P, D_IN], BF16)
         nc.sync.dma_start(out=x0_sb[:], in_=x0_rows)
         bw_rows = keep.tile([P, P], BF16)
@@ -124,8 +140,6 @@ def tile_fourierkartlayer_k_kernel(tc, X0, t, Wc_w_words, Wc_w_scales, Wc_b, w, 
         cos_codes = keep.tile([P, PASSES * P], U32, align_bytes=64)
         cos_scales = keep.tile([P, PASSES * P], U8, align_bytes=64)
         width = GROUP * P * 2
-        live = {}
-
         def load_w(grp):
             w_sb = wload.tile([P, GROUP * 2 * P], U32, align_bytes=64, name="w_sb")
             nc.sync.dma_start(out=w_sb[:].bitcast(I32), in_=w_words[:, grp * GROUP * 2 * P : (grp + 1) * GROUP * 2 * P])
@@ -217,16 +231,9 @@ def tile_fourierkartlayer_k_kernel(tc, X0, t, Wc_w_words, Wc_w_scales, Wc_b, w, 
         acc = ps_acc.tile([P, D_OUT], F32)
 
         def load_unit(k):
-            g, half = divmod(k, UNITS_PER_PASS)
-            d_rows = slice(half * PAIR * P, (half + 1) * PAIR * P)
-            qk_cols = slice(g * K_PASS, (g + 1) * K_PASS)
-            for name, source in (("bp_sb", bp_rows), ("a_sb", a_rows)):
-                sb = load.tile([P, PAIR * K_PASS], BF16, name=name)
-                nc.sync.dma_start(
-                    out=sb[:].rearrange("p (j c) -> p j c", j=PAIR),
-                    in_=source[d_rows, qk_cols].rearrange("(j p) c -> p j c", p=P),
-                )
-                live[name, k] = sb
+            if k > 0:
+                load_rows("bp_sb", bp_rows, k)
+            load_rows("a_sb", a_rows, k)
 
         def count_turns(k):
             phases = live["bp_sb", k][:]
@@ -269,11 +276,11 @@ def tile_fourierkartlayer_k_kernel(tc, X0, t, Wc_w_words, Wc_w_scales, Wc_b, w, 
 
         def transpose_y(k):
             for j in range(PAIR):
-                y_ps = ps_y.tile([P, PACK, P], F32, name="y_ps")
+                y_ps = ps_y.tile([P, P, PACK], F32, name="y_ps")
                 for u in range(2):
                     for e in range(HARM):
                         c0 = j * K_PASS + u * 2 * P + e
-                        y_block = y_ps[:, 2 * u + e, :]
+                        y_block = y_ps[:, :, 2 * u + e]
                         alone = c0 >= WIDE_END
                         if c0 < PLAIN_END:
                             bp_sb = live["bp_sb", k]
@@ -303,9 +310,9 @@ def tile_fourierkartlayer_k_kernel(tc, X0, t, Wc_w_words, Wc_w_scales, Wc_b, w, 
             sin_cos = trig.tile([P, 2, PAIR, K_PASS], F32, name="sin_cos", bufs=3)
             abs_b = trig.tile([P, PAIR, K_PASS], F32, name="abs_b")
             for j in range(PAIR):
-                y_t = live["y_ps", k, j][:].rearrange("p t d -> p d t")
-                nc.scalar.activation(out=sin_cos[:, 0, j, :].rearrange("p (d t) -> p d t", t=PACK), in_=y_t, func=ACT.Sin)
-                nc.scalar.activation(out=abs_b[:, j, :].rearrange("p (d t) -> p d t", t=PACK), in_=y_t, func=ACT.Abs)
+                flat = live["y_ps", k, j][:].rearrange("p d t -> p (d t)")
+                nc.scalar.activation(out=sin_cos[:, 0, j, :], in_=flat, func=ACT.Sin)
+                nc.scalar.activation(out=abs_b[:, j, :], in_=flat, func=ACT.Abs)
             live["sin_cos", k] = sin_cos
             live["abs_b", k] = abs_b
 
@@ -359,10 +366,13 @@ def tile_fourierkartlayer_k_kernel(tc, X0, t, Wc_w_words, Wc_w_scales, Wc_b, w, 
                 stop=(g == PASSES - 1),
             )
 
+        def due(step, lead):
+            return [k for k in range(UNITS) if step + lead == (k - HEAD if k < EARLY else k)]
+
         for step in range(-UNITS_PER_GROUP - ROWS_LEAD, UNITS + 2):
             ahead, part = divmod(step + ROWS_LEAD, UNITS_PER_GROUP)
-            if 0 <= step + 6 < UNITS:
-                load_unit(step + 6)
+            for k in due(step, 6):
+                load_unit(k)
             if part == 0 and 0 <= ahead + 1 < GROUPS:
                 load_w(ahead + 1)
             if step >= 3 and (step - 3) % UNITS_PER_PASS == 0:
@@ -371,19 +381,19 @@ def tile_fourierkartlayer_k_kernel(tc, X0, t, Wc_w_words, Wc_w_scales, Wc_b, w, 
                 first_matmul(ahead)
             if 0 <= step + 1 < UNITS:
                 transpose_a(step + 1)
-            if 0 <= step + 3 < UNITS:
-                reduce_phases(step + 3)
-            if 0 <= step + 4 < UNITS:
-                count_turns(step + 4)
-            if 0 <= step + 3 < UNITS:
-                transpose_y(step + 3)
+            for k in due(step, 3):
+                reduce_phases(k)
+            for k in due(step, 4):
+                count_turns(k)
+            for k in due(step, 3):
+                transpose_y(k)
             piece_group, piece = divmod(step + ROWS_LEAD - 2, UNITS_PER_GROUP)
             if 0 <= piece_group < GROUPS:
                 row_turns(piece_group, piece)
-            if 0 <= step + 2 < UNITS:
-                phase_sines(step + 2)
-            if 0 <= step + 1 < UNITS:
-                phase_cosines(step + 1)
+            for k in due(step, 2):
+                phase_sines(k)
+            for k in due(step, 1):
+                phase_cosines(k)
             if part == 3 and 0 <= ahead - 1 < GROUPS:
                 row_magnitudes(ahead - 1)
             if part == 0 and 0 <= ahead - 2 < GROUPS:

@@ -32,15 +32,12 @@ PAIR = 2
 UNITS_PER_PASS = D_BLOCKS // PAIR
 WORDS = K_PASS // HARM
 
-QUARTER = PAIR * K_PASS // 4
-PLAIN_END = QUARTER
-WIDE_END = 2 * QUARTER
-
-UNITS = PASSES * UNITS_PER_PASS
-UNITS_PER_GROUP = GROUP * UNITS_PER_PASS
-EARLY = 2
-HEAD = 4
-ROWS_LEAD = 8
+PLAIN = 1
+WIDE = 2
+EARLY = 1
+HEAD = 2
+PREFETCH = 5
+ROWS_LEAD = 4
 
 TWO_PI = 2.0 * math.pi
 HALF_PI = 0.5 * math.pi
@@ -63,7 +60,7 @@ def tile_fourierkartlayer_k_kernel(tc, X0, t, Wc_w_words, Wc_w_scales, Wc_b, w, 
         keep = stack.enter_context(tc.tile_pool(name="keep", bufs=1))
         wload = stack.enter_context(tc.tile_pool(name="wload", bufs=2))
         rows = stack.enter_context(tc.tile_pool(name="rows", bufs=1))
-        load = stack.enter_context(tc.tile_pool(name="load", bufs=7))
+        load = stack.enter_context(tc.tile_pool(name="load", bufs=5))
         handoff = stack.enter_context(tc.tile_pool(name="handoff", bufs=1))
         args = stack.enter_context(tc.tile_pool(name="args", bufs=2))
         trig = stack.enter_context(tc.tile_pool(name="trig", bufs=2))
@@ -81,16 +78,11 @@ def tile_fourierkartlayer_k_kernel(tc, X0, t, Wc_w_words, Wc_w_scales, Wc_b, w, 
 
         live = {}
 
-        def load_rows(name, source, k):
-            g, half = divmod(k, UNITS_PER_PASS)
-            d_rows = slice(half * PAIR * P, (half + 1) * PAIR * P)
+        def load_rows(name, source, g):
+            sb = load.tile([P, D_BLOCKS, K_PASS], BF16, name=name)
             qk_cols = slice(g * K_PASS, (g + 1) * K_PASS)
-            sb = load.tile([P, PAIR * K_PASS], BF16, name=name)
-            nc.sync.dma_start(
-                out=sb[:].rearrange("p (j c) -> p j c", j=PAIR),
-                in_=source[d_rows, qk_cols].rearrange("(j p) c -> p j c", p=P),
-            )
-            live[name, k] = sb
+            nc.sync.dma_start(out=sb[:], in_=source[:, qk_cols].rearrange("(j p) c -> p j c", p=P))
+            live[name, g] = sb
 
         load_rows("bp_sb", bp_rows, 0)
         x0_sb = keep.tile([P, D_IN], BF16)
@@ -135,10 +127,8 @@ def tile_fourierkartlayer_k_kernel(tc, X0, t, Wc_w_words, Wc_w_scales, Wc_b, w, 
         x0_scales = keep.tile([P, P], U8, align_bytes=64)
         nc.vector.quantize_mx(out=x0_codes[:].bitcast(FP8X4), scales=x0_scales[:], in_=x0_grouped[:])
 
-        sin_codes = keep.tile([P, PASSES * P], U32, align_bytes=64)
-        sin_scales = keep.tile([P, PASSES * P], U8, align_bytes=64)
-        cos_codes = keep.tile([P, PASSES * P], U32, align_bytes=64)
-        cos_scales = keep.tile([P, PASSES * P], U8, align_bytes=64)
+        row_codes = keep.tile([P, GROUPS, HARM, GROUP, P], U32, align_bytes=64)
+        row_scales = keep.tile([P, GROUPS, HARM, GROUP, P], U8, align_bytes=64)
         width = GROUP * P * 2
         def load_w(grp):
             w_sb = wload.tile([P, GROUP * 2 * P], U32, align_bytes=64, name="w_sb")
@@ -174,20 +164,20 @@ def tile_fourierkartlayer_k_kernel(tc, X0, t, Wc_w_words, Wc_w_scales, Wc_b, w, 
                 )
             live["angle", grp] = angle
 
-        def row_turns(grp, piece):
-            e, gl = divmod(piece, GROUP)
-            if piece == 0:
-                live["row_turns", grp] = rows.tile([P, HARM, GROUP, P * 2], I32, name="row_turns", bufs=2)
-            whole_turns(nc, live["row_turns", grp][:, e, gl, :], live["angle", grp][:, gl, :], (e + 1) / TWO_PI)
+        def row_turns(grp, e):
+            if e == 0:
+                live["row_turns", grp] = rows.tile([P, HARM, width], I32, name="row_turns", bufs=2)
+            angle = live["angle", grp][:].rearrange("p g c -> p (g c)")
+            whole_turns(nc, live["row_turns", grp][:, e, :], angle, (e + 1) / TWO_PI)
 
         def row_reduce(grp, e):
             if e == 0:
-                live["row_y", grp] = rows.tile([P, HARM, width], F32, name="row_y")
+                live["row_y", grp] = rows.tile([P, HARM, width], F32, name="row_y", bufs=2)
             nc.vector.scalar_tensor_tensor(
                 out=live["row_y", grp][:, e, :],
                 in0=live["angle", grp][:].rearrange("p g c -> p (g c)"),
                 scalar=(e + 1) / TWO_PI,
-                in1=live["row_turns", grp][:, e, :, :].rearrange("p g c -> p (g c)"),
+                in1=live["row_turns", grp][:, e, :],
                 op0=ALU.mult,
                 op1=ALU.subtract,
             )
@@ -200,97 +190,103 @@ def tile_fourierkartlayer_k_kernel(tc, X0, t, Wc_w_words, Wc_w_scales, Wc_b, w, 
 
         def row_sines(grp):
             y = live["row_y", grp]
-            sin_bf = rows.tile([P, width * HARM], BF16, align_bytes=64, name="sin_bf")
+            row_bf = rows.tile([P, 2, width * HARM], BF16, align_bytes=64, name="row_bf")
             nc.scalar.activation(
-                out=sin_bf[:].rearrange("p (c e) -> p c e", e=HARM),
+                out=row_bf[:, 0, :].rearrange("p (c e) -> p c e", e=HARM),
                 in_=y[:].rearrange("p e c -> p c e"),
                 func=ACT.Sin,
                 scale=TWO_PI,
             )
-            live["sin_bf", grp] = sin_bf
+            live["row_bf", grp] = row_bf
 
         def row_cosines(grp):
             y_abs = live["row_abs", grp]
-            cos_bf = rows.tile([P, width * HARM], BF16, align_bytes=64, name="cos_bf")
             nc.scalar.activation(
-                out=cos_bf[:].rearrange("p (c e) -> p c e", e=HARM),
+                out=live["row_bf", grp][:, 1, :].rearrange("p (c e) -> p c e", e=HARM),
                 in_=y_abs[:].rearrange("p e c -> p c e"),
                 func=ACT.Sin,
                 scale=-TWO_PI,
                 bias=HALF_PI,
             )
-            live["cos_bf", grp] = cos_bf
 
         def quantise_rows(grp):
-            cols = slice(grp * GROUP * P, (grp + 1) * GROUP * P)
-            sin_bf = live["sin_bf", grp]
-            cos_bf = live["cos_bf", grp]
-            nc.vector.quantize_mx(out=sin_codes[:, cols].bitcast(FP8X4), scales=sin_scales[:, cols], in_=sin_bf[:])
-            nc.vector.quantize_mx(out=cos_codes[:, cols].bitcast(FP8X4), scales=cos_scales[:, cols], in_=cos_bf[:])
+            nc.vector.quantize_mx(
+                out=row_codes[:, grp, :, :, :].rearrange("p f g r -> p (f g r)").bitcast(FP8X4),
+                scales=row_scales[:, grp, :, :, :].rearrange("p f g r -> p (f g r)"),
+                in_=live["row_bf", grp][:].rearrange("p f c -> p (f c)"),
+            )
 
         acc = ps_acc.tile([P, D_OUT], F32)
 
-        def load_unit(k):
-            if k > 0:
-                load_rows("bp_sb", bp_rows, k)
-            load_rows("a_sb", a_rows, k)
+        def load_pass(g):
+            if g > 0:
+                load_rows("bp_sb", bp_rows, g)
+            load_rows("a_sb", a_rows, g)
 
-        def count_turns(k):
-            phases = live["bp_sb", k][:]
-            turns = handoff.tile([P, PAIR * K_PASS], I32, name="phase_turns")
-            whole_turns(nc, turns[:], phases, 1.0 / TWO_PI)
-            live["turns", k] = turns
-            wide = args.tile([P, WIDE_END - PLAIN_END], F32, name="wide")
+        def count_turns(g):
+            turns = handoff.tile([P, D_BLOCKS, K_PASS], I32, name="phase_turns")
+            whole_turns(nc, turns[:], live["bp_sb", g][:], 1.0 / TWO_PI)
+            live["turns", g] = turns
+
+        def widen_phases(g):
+            wide = args.tile([P, WIDE, K_PASS], F32, name="wide")
             nc.gpsimd.tensor_scalar(
-                out=wide[:], in0=phases[:, PLAIN_END:WIDE_END], scalar1=1.0, scalar2=0.0, op0=ALU.mult, op1=ALU.add
-            )
-            live["wide", k] = wide
-
-        def reduce_phases(k):
-            turns = live["turns", k]
-            reduced = args.tile([P, PAIR * K_PASS], F32, name="reduced")
-            nc.vector.tensor_scalar(
-                out=reduced[:, :WIDE_END], in0=turns[:, :WIDE_END], scalar1=-TWO_PI, scalar2=None, op0=ALU.mult
-            )
-            nc.vector.scalar_tensor_tensor(
-                out=reduced[:, WIDE_END:],
-                in0=turns[:, WIDE_END:],
-                scalar=-TWO_PI,
-                in1=live["bp_sb", k][:, WIDE_END:],
+                out=wide[:],
+                in0=live["bp_sb", g][:, PLAIN : PLAIN + WIDE, :],
+                scalar1=1.0,
+                scalar2=0.0,
                 op0=ALU.mult,
                 op1=ALU.add,
             )
-            live["reduced", k] = reduced
+            live["wide", g] = wide
 
-        def transpose_a(k):
-            a_words = live["a_sb", k][:].bitcast(F32)
+        def reduce_phases(g):
+            turns = live["turns", g]
+            reduced = args.tile([P, D_BLOCKS, K_PASS], F32, name="reduced")
+            summed = PLAIN + WIDE
+            nc.vector.tensor_scalar(
+                out=reduced[:, :summed, :], in0=turns[:, :summed, :], scalar1=-TWO_PI, scalar2=None, op0=ALU.mult
+            )
+            nc.vector.scalar_tensor_tensor(
+                out=reduced[:, summed:, :],
+                in0=turns[:, summed:, :],
+                scalar=-TWO_PI,
+                in1=live["bp_sb", g][:, summed:, :],
+                op0=ALU.mult,
+                op1=ALU.add,
+            )
+            live["reduced", g] = reduced
+
+        def transpose_a(g, half):
+            a_words = live["a_sb", g][:].rearrange("p j c -> p (j c)").bitcast(F32)
             a_ps = ps_a.tile([P, PAIR, P, 2], F32, name="a_ps")
             for j in range(PAIR):
                 for u in range(2):
-                    m0 = j * WORDS + u * P
+                    m0 = (half * PAIR + j) * WORDS + u * P
                     nc.tensor.transpose(a_ps[:, j, :, u], a_words[:, m0 : m0 + P], ident[:])
-            live["a_ps", k] = a_ps
+            live["a_ps", g, half] = a_ps
 
-        def every_second(tile, c0):
-            return tile[:, c0 : c0 + 2 * P - 1 : 2]
-
-        def transpose_y(k):
+        def transpose_y(g, half):
             for j in range(PAIR):
+                block = half * PAIR + j
                 y_ps = ps_y.tile([P, P, PACK], F32, name="y_ps")
                 for u in range(2):
                     for e in range(HARM):
-                        c0 = j * K_PASS + u * 2 * P + e
+                        cols = slice(u * 2 * P + e, (u + 1) * 2 * P - 1 + e, 2)
                         y_block = y_ps[:, :, 2 * u + e]
-                        alone = c0 >= WIDE_END
-                        if c0 < PLAIN_END:
-                            bp_sb = live["bp_sb", k]
+                        alone = block >= PLAIN + WIDE
+                        if block < PLAIN:
                             nc.tensor.matmul(
-                                out=y_block, lhsT=every_second(bp_sb, c0), rhs=ident_bf[:], start=True, stop=False
+                                out=y_block,
+                                lhsT=live["bp_sb", g][:, block, cols],
+                                rhs=ident_bf[:],
+                                start=True,
+                                stop=False,
                             )
                         elif not alone:
                             nc.tensor.matmul(
                                 out=y_block,
-                                lhsT=every_second(live["wide", k], c0 - PLAIN_END),
+                                lhsT=live["wide", g][:, block - PLAIN, cols],
                                 rhs=ident[:],
                                 is_transpose=True,
                                 start=True,
@@ -298,120 +294,118 @@ def tile_fourierkartlayer_k_kernel(tc, X0, t, Wc_w_words, Wc_w_scales, Wc_b, w, 
                             )
                         nc.tensor.matmul(
                             out=y_block,
-                            lhsT=every_second(live["reduced", k], c0),
+                            lhsT=live["reduced", g][:, block, cols],
                             rhs=ident[:],
                             is_transpose=True,
                             start=alone,
                             stop=True,
                         )
-                live["y_ps", k, j] = y_ps
+                live["y_ps", g, block] = y_ps
 
-        def phase_sines(k):
-            sin_cos = trig.tile([P, 2, PAIR, K_PASS], F32, name="sin_cos", bufs=3)
+        def phase_sines(g, half):
+            sin_cos = trig.tile([P, 2, PAIR, K_PASS], F32, name="sin_cos", bufs=4)
             abs_b = trig.tile([P, PAIR, K_PASS], F32, name="abs_b")
             for j in range(PAIR):
-                flat = live["y_ps", k, j][:].rearrange("p d t -> p (d t)")
+                flat = live["y_ps", g, half * PAIR + j][:].rearrange("p d t -> p (d t)")
                 nc.scalar.activation(out=sin_cos[:, 0, j, :], in_=flat, func=ACT.Sin)
                 nc.scalar.activation(out=abs_b[:, j, :], in_=flat, func=ACT.Abs)
-            live["sin_cos", k] = sin_cos
-            live["abs_b", k] = abs_b
+            live["sin_cos", g, half] = sin_cos
+            live["abs_b", g, half] = abs_b
 
-        def phase_cosines(k):
+        def phase_cosines(g, half):
             nc.scalar.activation(
-                out=live["sin_cos", k][:, 1, :, :], in_=live["abs_b", k][:], func=ACT.Sin, scale=-1.0, bias=HALF_PI
+                out=live["sin_cos", g, half][:, 1, :, :],
+                in_=live["abs_b", g, half][:],
+                func=ACT.Sin,
+                scale=-1.0,
+                bias=HALF_PI,
             )
 
-        def multiply(k):
-            a_t = live["a_ps", k][:].rearrange("p j d u -> p (j d u)").bitcast(BF16)
-            products = trig.tile([P, 2, PAIR * K_PASS], BF16, align_bytes=64, name="products")
+        def multiply(g, half):
+            a_t = live["a_ps", g, half][:].rearrange("p j d u -> p (j d u)").bitcast(BF16)
+            if half == 0:
+                live["products", g] = trig.tile([P, 2, D_BLOCKS * K_PASS], BF16, align_bytes=64, name="products")
+            unit_cols = slice(half * PAIR * K_PASS, (half + 1) * PAIR * K_PASS)
             nc.vector.tensor_tensor(
-                out=products[:],
-                in0=live["sin_cos", k][:].rearrange("p f j c -> p f (j c)"),
+                out=live["products", g][:, :, unit_cols],
+                in0=live["sin_cos", g, half][:].rearrange("p f j c -> p f (j c)"),
                 in1=a_t.unsqueeze(1).to_broadcast([P, 2, PAIR * K_PASS]),
                 op=ALU.mult,
             )
-            live["products", k] = products
 
-        def quantise(k):
-            g, half = divmod(k, UNITS_PER_PASS)
-            d_cols = slice(half * PAIR * P, (half + 1) * PAIR * P)
-            for f, name in enumerate(("asin", "acos")):
-                if half == 0:
-                    live[name + "_codes", g] = codes.tile([P, D_OUT], U32, align_bytes=64, name=name + "_codes")
-                    live[name + "_scales", g] = codes.tile([P, D_OUT], U8, align_bytes=64, name=name + "_scales")
-                nc.vector.quantize_mx(
-                    out=live[name + "_codes", g][:, d_cols].bitcast(FP8X4),
-                    scales=live[name + "_scales", g][:, d_cols],
-                    in_=live["products", k][:, f, :],
-                )
-
-        def long_sums(g):
-            r_cols = slice(g * P, (g + 1) * P)
-            nc.tensor.matmul_mx(
-                out=acc[:],
-                lhsT=sin_codes[:, r_cols].bitcast(FP8X4),
-                lhsT_scale=sin_scales[:, r_cols],
-                rhs=live["acos_codes", g][:].bitcast(FP8X4),
-                rhs_scale=live["acos_scales", g][:],
-                start=(g == 0),
-                stop=False,
+        def quantise(g, f):
+            w_codes = codes.tile([P, D_OUT], U32, align_bytes=64, name="w_codes", bufs=4)
+            w_code_scales = codes.tile([P, D_OUT], U8, align_bytes=64, name="w_code_scales", bufs=4)
+            nc.vector.quantize_mx(
+                out=w_codes[:].bitcast(FP8X4), scales=w_code_scales[:], in_=live["products", g][:, f, :]
             )
+            live["w_codes", g, f] = (w_codes, w_code_scales)
+
+        def long_sum(g, f):
+            grp, gl = divmod(g, GROUP)
+            w_codes, w_code_scales = live["w_codes", g, f]
             nc.tensor.matmul_mx(
                 out=acc[:],
-                lhsT=cos_codes[:, r_cols].bitcast(FP8X4),
-                lhsT_scale=cos_scales[:, r_cols],
-                rhs=live["asin_codes", g][:].bitcast(FP8X4),
-                rhs_scale=live["asin_scales", g][:],
-                start=False,
-                stop=(g == PASSES - 1),
+                lhsT=row_codes[:, grp, 1 - f, gl, :].bitcast(FP8X4),
+                lhsT_scale=row_scales[:, grp, 1 - f, gl, :],
+                rhs=w_codes[:].bitcast(FP8X4),
+                rhs_scale=w_code_scales[:],
+                start=(g == 0 and f == 0),
+                stop=(g == PASSES - 1 and f == 1),
             )
 
         def due(step, lead):
-            return [k for k in range(UNITS) if step + lead == (k - HEAD if k < EARLY else k)]
+            return [g for g in range(PASSES) if step + lead == (g - HEAD if g < EARLY else g)]
 
-        for step in range(-UNITS_PER_GROUP - ROWS_LEAD, UNITS + 2):
-            ahead, part = divmod(step + ROWS_LEAD, UNITS_PER_GROUP)
-            for k in due(step, 6):
-                load_unit(k)
-            if part == 0 and 0 <= ahead + 1 < GROUPS:
-                load_w(ahead + 1)
-            if step >= 3 and (step - 3) % UNITS_PER_PASS == 0:
-                long_sums((step - 3) // UNITS_PER_PASS)
-            if part == 0 and 0 <= ahead < GROUPS:
-                first_matmul(ahead)
-            if 0 <= step + 1 < UNITS:
-                transpose_a(step + 1)
-            for k in due(step, 3):
-                reduce_phases(k)
-            for k in due(step, 4):
-                count_turns(k)
-            for k in due(step, 3):
-                transpose_y(k)
-            piece_group, piece = divmod(step + ROWS_LEAD - 2, UNITS_PER_GROUP)
-            if 0 <= piece_group < GROUPS:
-                row_turns(piece_group, piece)
-            for k in due(step, 2):
-                phase_sines(k)
-            for k in due(step, 1):
-                phase_cosines(k)
-            if part == 3 and 0 <= ahead - 1 < GROUPS:
-                row_magnitudes(ahead - 1)
-            if part == 0 and 0 <= ahead - 2 < GROUPS:
-                row_sines(ahead - 2)
-            if part == 1 and 0 <= ahead - 2 < GROUPS:
-                row_cosines(ahead - 2)
-            if 0 <= step < UNITS:
-                multiply(step)
-            if part == 1 and 0 <= ahead < GROUPS:
-                row_angles(ahead)
-            if 0 <= step - 1 < UNITS:
-                quantise(step - 1)
-            if part == 1 and 0 <= ahead - 1 < GROUPS:
-                row_reduce(ahead - 1, 0)
-            if part == 2 and 0 <= ahead - 1 < GROUPS:
-                row_reduce(ahead - 1, 1)
-            if part == 2 and 0 <= ahead - 2 < GROUPS:
-                quantise_rows(ahead - 2)
+        for step in range(-PREFETCH - HEAD, PASSES + 2):
+
+            def row_stage(stage, steps, *more):
+                grp, rest = divmod(step + ROWS_LEAD - steps, GROUP)
+                if rest == 0 and 0 <= grp < GROUPS:
+                    stage(grp, *more)
+
+            for g in due(step, PREFETCH):
+                load_pass(g)
+            row_stage(load_w, -GROUP)
+            if 0 <= step - 1 < PASSES:
+                for f in range(2):
+                    quantise(step - 1, f)
+            if step < 0:
+                for g in due(step, 2):
+                    reduce_phases(g)
+            row_stage(row_reduce, 2, 0)
+            row_stage(row_reduce, 3, 1)
+            row_stage(quantise_rows, 5)
+            if step >= 0:
+                for g in due(step, 2):
+                    reduce_phases(g)
+            for g in due(step, 3):
+                count_turns(g)
+                widen_phases(g)
+            row_stage(row_turns, 1, 0)
+            row_stage(row_turns, 2, 1)
+            for g in due(step, 1):
+                phase_sines(g, 0)
+            for g in due(step, 0):
+                phase_cosines(g, 1)
+            row_stage(row_sines, 4)
+            for g in due(step, 1):
+                phase_sines(g, 1)
+                phase_cosines(g, 0)
+            row_stage(row_magnitudes, 3)
+            row_stage(row_cosines, 4)
+            row_stage(first_matmul, 0)
+            for half in range(UNITS_PER_PASS):
+                for g in due(step, 2):
+                    transpose_y(g, half)
+                if 0 <= step < PASSES:
+                    multiply(step, half)
+                if 0 <= step + 1 < PASSES:
+                    transpose_a(step + 1, half)
+            row_stage(row_angles, 0)
+            if 0 <= step - 1 < PASSES:
+                for f in range(2):
+                    long_sum(step - 1, f)
 
         result = keep.tile([P, D_OUT], F32)
         nc.vector.tensor_copy(out=result[:], in_=acc[:])

@@ -34,8 +34,9 @@ WORDS = K_PASS // HARM
 
 PLAIN = 1
 WIDE = 2
-EARLY = 1
-HEAD = 2
+SUMMED = PLAIN + WIDE
+FIRST = 2
+FOLD = 256
 PREFETCH = 5
 ROWS_LEAD = 4
 
@@ -76,6 +77,9 @@ def tile_fourierkartlayer_k_kernel(tc, X0, t, Wc_w_words, Wc_w_scales, Wc_b, w, 
         ident_bf = keep.tile([P, P], BF16)
         make_identity(nc, ident_bf[:])
 
+        w_scales = keep.tile([P, Q], U8, align_bytes=64)
+        nc.vector.memset(w_scales[:].bitcast(I32), 0)
+
         live = {}
 
         def load_rows(name, source, g):
@@ -92,30 +96,97 @@ def tile_fourierkartlayer_k_kernel(tc, X0, t, Wc_w_words, Wc_w_scales, Wc_b, w, 
         nc.sync.dma_start(out=bw_rows[Q_BLOCKS:P, :], in_=w.rearrange("(j p) -> j p", p=P))
         t_bf = keep.tile([P, 2], BF16)
         nc.sync.dma_start(out=t_bf[:], in_=t.rearrange("b o -> (b o)").partition_broadcast(P))
-        w_scales = keep.tile([P, Q], U8, align_bytes=64)
-        nc.vector.memset(w_scales[:].bitcast(I32), 0)
         for quad in range(4):
             nc.sync.dma_start(
                 out=w_scales[32 * quad : 32 * quad + 4, :].bitcast(I32),
                 in_=Wc_w_scales[0, 4 * quad : 4 * quad + 4, :].bitcast(I32),
             )
-        t_f32 = keep.tile([P, 2], F32)
-        nc.vector.tensor_copy(out=t_f32[:], in_=t_bf[:])
 
-        bw_ps = ps_c.tile([P, P], BF16, tag="c")
-        nc.tensor.transpose(bw_ps[:], bw_rows[:], ident_bf[:])
-        bw = keep.tile([P, P], F32)
-        nc.vector.tensor_copy(out=bw[:], in_=bw_ps[:])
-        shift = keep.tile([P, Q_BLOCKS, 2], F32)
-        for b in range(2):
+        def load_w(grp):
+            w_sb = wload.tile([P, GROUP * 2 * P], U32, align_bytes=64, name="w_sb")
+            nc.sync.dma_start(out=w_sb[:].bitcast(I32), in_=w_words[:, grp * GROUP * 2 * P : (grp + 1) * GROUP * 2 * P])
+            live["w_sb", grp] = w_sb
+
+        load_w(0)
+        load_rows("bp_sb", bp_rows, 1)
+        load_rows("a_sb", a_rows, 0)
+        load_w(1)
+        load_rows("a_sb", a_rows, 1)
+
+        def spans(g):
+            return ((0, PAIR), (PAIR, D_BLOCKS)) if g == 0 else ((0, D_BLOCKS),)
+
+        def count_turns(g):
+            phases = live["bp_sb", g]
+            turns = handoff.tile([P, D_BLOCKS, K_PASS], I32, name="phase_turns")
+            wide = args.tile([P, WIDE, K_PASS], F32, name="wide")
+            for lo, hi in spans(g):
+                whole_turns(nc, turns[:, lo:hi, :], phases[:, lo:hi, :], 1.0 / TWO_PI)
+                first, end = max(lo, PLAIN), min(hi, SUMMED)
+                nc.gpsimd.tensor_scalar(
+                    out=wide[:, first - PLAIN : end - PLAIN, :],
+                    in0=phases[:, first:end, :],
+                    scalar1=1.0,
+                    scalar2=0.0,
+                    op0=ALU.mult,
+                    op1=ALU.add,
+                )
+            live["turns", g] = turns
+            live["wide", g] = wide
+
+        def reduce_phases(g):
+            turns = live["turns", g]
+            reduced = args.tile([P, D_BLOCKS, K_PASS], F32, name="reduced")
+            live["reduced", g] = reduced
+            for lo, hi in spans(g):
+                end = min(hi, SUMMED)
+                nc.vector.tensor_scalar(
+                    out=reduced[:, lo:end, :], in0=turns[:, lo:end, :], scalar1=-TWO_PI, scalar2=None, op0=ALU.mult
+                )
             nc.vector.scalar_tensor_tensor(
-                out=shift[:, :, b],
-                in0=bw[:, Q_BLOCKS:P],
-                scalar=t_f32[:, b : b + 1],
-                in1=bw[:, 0:Q_BLOCKS],
+                out=reduced[:, SUMMED:, :],
+                in0=turns[:, SUMMED:, :],
+                scalar=-TWO_PI,
+                in1=live["bp_sb", g][:, SUMMED:, :],
                 op0=ALU.mult,
                 op1=ALU.add,
             )
+
+        def transpose_y(g, half):
+            for j in range(PAIR):
+                block = half * PAIR + j
+                y_ps = ps_y.tile([P, P, PACK], F32, name="y_ps")
+                for u in range(2):
+                    for e in range(HARM):
+                        cols = slice(u * 2 * P + e, (u + 1) * 2 * P - 1 + e, 2)
+                        y_block = y_ps[:, :, 2 * u + e]
+                        alone = block >= SUMMED
+                        if block < PLAIN:
+                            nc.tensor.matmul(
+                                out=y_block,
+                                lhsT=live["bp_sb", g][:, block, cols],
+                                rhs=ident_bf[:],
+                                start=True,
+                                stop=False,
+                            )
+                        elif not alone:
+                            nc.tensor.matmul(
+                                out=y_block,
+                                lhsT=live["wide", g][:, block - PLAIN, cols],
+                                rhs=ident[:],
+                                is_transpose=True,
+                                start=True,
+                                stop=False,
+                            )
+                        nc.tensor.matmul(
+                            out=y_block,
+                            lhsT=live["reduced", g][:, block, cols],
+                            rhs=ident[:],
+                            is_transpose=True,
+                            start=alone,
+                            stop=True,
+                        )
+                live["y_ps", g, block] = y_ps
 
         x0_words = x0_sb[:].bitcast(F32)
         x0_ps = ps_c.tile([P, P, 2], F32, tag="c")
@@ -127,14 +198,30 @@ def tile_fourierkartlayer_k_kernel(tc, X0, t, Wc_w_words, Wc_w_scales, Wc_b, w, 
         x0_scales = keep.tile([P, P], U8, align_bytes=64)
         nc.vector.quantize_mx(out=x0_codes[:].bitcast(FP8X4), scales=x0_scales[:], in_=x0_grouped[:])
 
+        count_turns(0)
+        reduce_phases(0)
+        for half in range(UNITS_PER_PASS):
+            transpose_y(0, half)
+        count_turns(1)
+
+        bw_ps = ps_c.tile([P, P], BF16, tag="c")
+        nc.tensor.transpose(bw_ps[:], bw_rows[:], ident_bf[:])
+        b_cols = keep.tile([P, Q_BLOCKS], F32)
+        nc.vector.tensor_copy(out=b_cols[:], in_=bw_ps[:, 0:Q_BLOCKS])
+        shift = keep.tile([P, Q_BLOCKS, 2], F32)
+        for b in range(2):
+            nc.vector.scalar_tensor_tensor(
+                out=shift[:, :, b],
+                in0=bw_ps[:, Q_BLOCKS:P],
+                scalar=t_bf[:, b : b + 1],
+                in1=b_cols[:],
+                op0=ALU.mult,
+                op1=ALU.add,
+            )
+
         row_codes = keep.tile([P, GROUPS, HARM, GROUP, P], U32, align_bytes=64)
         row_scales = keep.tile([P, GROUPS, HARM, GROUP, P], U8, align_bytes=64)
         width = GROUP * P * 2
-        def load_w(grp):
-            w_sb = wload.tile([P, GROUP * 2 * P], U32, align_bytes=64, name="w_sb")
-            nc.sync.dma_start(out=w_sb[:].bitcast(I32), in_=w_words[:, grp * GROUP * 2 * P : (grp + 1) * GROUP * 2 * P])
-            live["w_sb", grp] = w_sb
-
         def first_matmul(grp):
             w_sb = live["w_sb", grp]
             c_ps = ps_c.tile([P, GROUP * 2, P], F32, name="c_ps", tag="c")
@@ -182,11 +269,15 @@ def tile_fourierkartlayer_k_kernel(tc, X0, t, Wc_w_words, Wc_w_scales, Wc_b, w, 
                 op1=ALU.subtract,
             )
 
+        def row_folds(grp):
+            row_a = rows.tile([P, HARM * width], F32, name="row_a", bufs=2)
+            y = live["row_y", grp][:, 0, :FOLD]
+            nc.vector.scalar_tensor_tensor(out=row_a[:, :FOLD], in0=y, scalar=-0.25, in1=y, op0=ALU.is_lt, op1=ALU.add)
+            live["row_a", grp] = row_a
+
         def row_magnitudes(grp):
-            y = live["row_y", grp]
-            y_abs = rows.tile([P, HARM, width], F32, name="row_abs")
-            nc.scalar.activation(out=y_abs[:], in_=y[:], func=ACT.Abs)
-            live["row_abs", grp] = y_abs
+            y = live["row_y", grp][:].rearrange("p e c -> p (e c)")
+            nc.scalar.activation(out=live["row_a", grp][:, FOLD:], in_=y[:, FOLD:], func=ACT.Abs)
 
         def row_sines(grp):
             y = live["row_y", grp]
@@ -200,10 +291,9 @@ def tile_fourierkartlayer_k_kernel(tc, X0, t, Wc_w_words, Wc_w_scales, Wc_b, w, 
             live["row_bf", grp] = row_bf
 
         def row_cosines(grp):
-            y_abs = live["row_abs", grp]
             nc.scalar.activation(
                 out=live["row_bf", grp][:, 1, :].rearrange("p (c e) -> p c e", e=HARM),
-                in_=y_abs[:].rearrange("p e c -> p c e"),
+                in_=live["row_a", grp][:].rearrange("p (e c) -> p c e", e=HARM),
                 func=ACT.Sin,
                 scale=-TWO_PI,
                 bias=HALF_PI,
@@ -216,46 +306,8 @@ def tile_fourierkartlayer_k_kernel(tc, X0, t, Wc_w_words, Wc_w_scales, Wc_b, w, 
                 in_=live["row_bf", grp][:].rearrange("p f c -> p (f c)"),
             )
 
+        last = PASSES - 1
         acc = ps_acc.tile([P, D_OUT], F32)
-
-        def load_pass(g):
-            if g > 0:
-                load_rows("bp_sb", bp_rows, g)
-            load_rows("a_sb", a_rows, g)
-
-        def count_turns(g):
-            turns = handoff.tile([P, D_BLOCKS, K_PASS], I32, name="phase_turns")
-            whole_turns(nc, turns[:], live["bp_sb", g][:], 1.0 / TWO_PI)
-            live["turns", g] = turns
-
-        def widen_phases(g):
-            wide = args.tile([P, WIDE, K_PASS], F32, name="wide")
-            nc.gpsimd.tensor_scalar(
-                out=wide[:],
-                in0=live["bp_sb", g][:, PLAIN : PLAIN + WIDE, :],
-                scalar1=1.0,
-                scalar2=0.0,
-                op0=ALU.mult,
-                op1=ALU.add,
-            )
-            live["wide", g] = wide
-
-        def reduce_phases(g):
-            turns = live["turns", g]
-            reduced = args.tile([P, D_BLOCKS, K_PASS], F32, name="reduced")
-            summed = PLAIN + WIDE
-            nc.vector.tensor_scalar(
-                out=reduced[:, :summed, :], in0=turns[:, :summed, :], scalar1=-TWO_PI, scalar2=None, op0=ALU.mult
-            )
-            nc.vector.scalar_tensor_tensor(
-                out=reduced[:, summed:, :],
-                in0=turns[:, summed:, :],
-                scalar=-TWO_PI,
-                in1=live["bp_sb", g][:, summed:, :],
-                op0=ALU.mult,
-                op1=ALU.add,
-            )
-            live["reduced", g] = reduced
 
         def transpose_a(g, half):
             a_words = live["a_sb", g][:].rearrange("p j c -> p (j c)").bitcast(F32)
@@ -265,42 +317,6 @@ def tile_fourierkartlayer_k_kernel(tc, X0, t, Wc_w_words, Wc_w_scales, Wc_b, w, 
                     m0 = (half * PAIR + j) * WORDS + u * P
                     nc.tensor.transpose(a_ps[:, j, :, u], a_words[:, m0 : m0 + P], ident[:])
             live["a_ps", g, half] = a_ps
-
-        def transpose_y(g, half):
-            for j in range(PAIR):
-                block = half * PAIR + j
-                y_ps = ps_y.tile([P, P, PACK], F32, name="y_ps")
-                for u in range(2):
-                    for e in range(HARM):
-                        cols = slice(u * 2 * P + e, (u + 1) * 2 * P - 1 + e, 2)
-                        y_block = y_ps[:, :, 2 * u + e]
-                        alone = block >= PLAIN + WIDE
-                        if block < PLAIN:
-                            nc.tensor.matmul(
-                                out=y_block,
-                                lhsT=live["bp_sb", g][:, block, cols],
-                                rhs=ident_bf[:],
-                                start=True,
-                                stop=False,
-                            )
-                        elif not alone:
-                            nc.tensor.matmul(
-                                out=y_block,
-                                lhsT=live["wide", g][:, block - PLAIN, cols],
-                                rhs=ident[:],
-                                is_transpose=True,
-                                start=True,
-                                stop=False,
-                            )
-                        nc.tensor.matmul(
-                            out=y_block,
-                            lhsT=live["reduced", g][:, block, cols],
-                            rhs=ident[:],
-                            is_transpose=True,
-                            start=alone,
-                            stop=True,
-                        )
-                live["y_ps", g, block] = y_ps
 
         def phase_sines(g, half):
             sin_cos = trig.tile([P, 2, PAIR, K_PASS], F32, name="sin_cos", bufs=4)
@@ -321,91 +337,106 @@ def tile_fourierkartlayer_k_kernel(tc, X0, t, Wc_w_words, Wc_w_scales, Wc_b, w, 
                 bias=HALF_PI,
             )
 
-        def multiply(g, half):
+        def multiply(g, half, f0, f1):
             a_t = live["a_ps", g, half][:].rearrange("p j d u -> p (j d u)").bitcast(BF16)
-            if half == 0:
+            if half == 0 and f0 == 0:
                 live["products", g] = trig.tile([P, 2, D_BLOCKS * K_PASS], BF16, align_bytes=64, name="products")
             unit_cols = slice(half * PAIR * K_PASS, (half + 1) * PAIR * K_PASS)
             nc.vector.tensor_tensor(
-                out=live["products", g][:, :, unit_cols],
-                in0=live["sin_cos", g, half][:].rearrange("p f j c -> p f (j c)"),
-                in1=a_t.unsqueeze(1).to_broadcast([P, 2, PAIR * K_PASS]),
+                out=live["products", g][:, f0:f1, unit_cols],
+                in0=live["sin_cos", g, half][:, f0:f1, :, :].rearrange("p f j c -> p f (j c)"),
+                in1=a_t.unsqueeze(1).to_broadcast([P, f1 - f0, PAIR * K_PASS]),
                 op=ALU.mult,
             )
 
-        def quantise(g, f):
-            w_codes = codes.tile([P, D_OUT], U32, align_bytes=64, name="w_codes", bufs=4)
-            w_code_scales = codes.tile([P, D_OUT], U8, align_bytes=64, name="w_code_scales", bufs=4)
+        def quantise(g, f0, f1):
+            if f0 == 0:
+                live["w_codes", g] = codes.tile([P, 2, D_OUT], U32, align_bytes=64, name="w_codes", bufs=3)
+                live["w_code_scales", g] = codes.tile([P, 2, D_OUT], U8, align_bytes=64, name="w_code_scales", bufs=3)
             nc.vector.quantize_mx(
-                out=w_codes[:].bitcast(FP8X4), scales=w_code_scales[:], in_=live["products", g][:, f, :]
+                out=live["w_codes", g][:, f0:f1, :].rearrange("p f d -> p (f d)").bitcast(FP8X4),
+                scales=live["w_code_scales", g][:, f0:f1, :].rearrange("p f d -> p (f d)"),
+                in_=live["products", g][:, f0:f1, :].rearrange("p f c -> p (f c)"),
             )
-            live["w_codes", g, f] = (w_codes, w_code_scales)
 
-        def long_sum(g, f):
+        def long_sum(g):
             grp, gl = divmod(g, GROUP)
-            w_codes, w_code_scales = live["w_codes", g, f]
-            nc.tensor.matmul_mx(
-                out=acc[:],
-                lhsT=row_codes[:, grp, 1 - f, gl, :].bitcast(FP8X4),
-                lhsT_scale=row_scales[:, grp, 1 - f, gl, :],
-                rhs=w_codes[:].bitcast(FP8X4),
-                rhs_scale=w_code_scales[:],
-                start=(g == 0 and f == 0),
-                stop=(g == PASSES - 1 and f == 1),
-            )
+            for f in range(2):
+                nc.tensor.matmul_mx(
+                    out=acc[:],
+                    lhsT=row_codes[:, grp, 1 - f, gl, :].bitcast(FP8X4),
+                    lhsT_scale=row_scales[:, grp, 1 - f, gl, :],
+                    rhs=live["w_codes", g][:, f, :].bitcast(FP8X4),
+                    rhs_scale=live["w_code_scales", g][:, f, :],
+                    start=(g == 0 and f == 0),
+                    stop=(g == last and f == 1),
+                )
+
+        first_matmul(0)
+        row_angles(0)
 
         def due(step, lead):
-            return [g for g in range(PASSES) if step + lead == (g - HEAD if g < EARLY else g)]
+            return [g for g in range(PASSES) if step + lead == (g - 1 if g < FIRST else g)]
 
-        for step in range(-PREFETCH - HEAD, PASSES + 2):
+        for step in range(1 - ROWS_LEAD, PASSES):
 
             def row_stage(stage, steps, *more):
                 grp, rest = divmod(step + ROWS_LEAD - steps, GROUP)
                 if rest == 0 and 0 <= grp < GROUPS:
                     stage(grp, *more)
 
-            for g in due(step, PREFETCH):
-                load_pass(g)
-            row_stage(load_w, -GROUP)
-            if 0 <= step - 1 < PASSES:
-                for f in range(2):
-                    quantise(step - 1, f)
+            row_stage(load_w, -GROUP - 1)
+            if step + PREFETCH < PASSES:
+                load_rows("bp_sb", bp_rows, step + PREFETCH)
+                load_rows("a_sb", a_rows, step + PREFETCH)
             if step < 0:
                 for g in due(step, 2):
-                    reduce_phases(g)
+                    if g > 0:
+                        reduce_phases(g)
             row_stage(row_reduce, 2, 0)
             row_stage(row_reduce, 3, 1)
-            row_stage(quantise_rows, 5)
+            row_stage(row_folds, 3)
+            row_stage(quantise_rows, 6)
+            if step >= 1:
+                quantise(step - 1, 0, 2)
             if step >= 0:
                 for g in due(step, 2):
                     reduce_phases(g)
-            for g in due(step, 3):
-                count_turns(g)
-                widen_phases(g)
+            if FIRST <= step + 3 < PASSES:
+                count_turns(step + 3)
             row_stage(row_turns, 1, 0)
             row_stage(row_turns, 2, 1)
             for g in due(step, 1):
                 phase_sines(g, 0)
             for g in due(step, 0):
                 phase_cosines(g, 1)
-            row_stage(row_sines, 4)
+            row_stage(row_magnitudes, 4)
+            row_stage(row_cosines, 5)
             for g in due(step, 1):
                 phase_sines(g, 1)
                 phase_cosines(g, 0)
-            row_stage(row_magnitudes, 3)
-            row_stage(row_cosines, 4)
-            row_stage(first_matmul, 0)
+            row_stage(row_sines, 4)
             for half in range(UNITS_PER_PASS):
                 for g in due(step, 2):
-                    transpose_y(g, half)
-                if 0 <= step < PASSES:
-                    multiply(step, half)
+                    if g > 0:
+                        transpose_y(g, half)
+                if 0 <= step < last:
+                    multiply(step, half, 0, 2)
+                if half == 0:
+                    row_stage(row_angles, 0)
                 if 0 <= step + 1 < PASSES:
                     transpose_a(step + 1, half)
-            row_stage(row_angles, 0)
-            if 0 <= step - 1 < PASSES:
-                for f in range(2):
-                    long_sum(step - 1, f)
+            if step >= 2:
+                long_sum(step - 2)
+            row_stage(first_matmul, -1)
+        for f in range(2):
+            for half in range(UNITS_PER_PASS):
+                multiply(last, half, f, f + 1)
+            quantise(last, f, f + 1)
+            if f == 0:
+                quantise_rows(GROUPS - 1)
+        long_sum(last - 1)
+        long_sum(last)
 
         result = keep.tile([P, D_OUT], F32)
         nc.vector.tensor_copy(out=result[:], in_=acc[:])

@@ -36,9 +36,9 @@ PLAIN = 1
 WIDE = 2
 SUMMED = PLAIN + WIDE
 FIRST = 2
-FOLD = 256
 PREFETCH = 5
-ROWS_LEAD = 4
+ROWS_LEAD = 3
+SUM_LAG = 4
 
 TWO_PI = 2.0 * math.pi
 HALF_PI = 0.5 * math.pi
@@ -219,8 +219,6 @@ def tile_fourierkartlayer_k_kernel(tc, X0, t, Wc_w_words, Wc_w_scales, Wc_b, w, 
                 op1=ALU.add,
             )
 
-        row_codes = keep.tile([P, GROUPS, HARM, GROUP, P], U32, align_bytes=64)
-        row_scales = keep.tile([P, GROUPS, HARM, GROUP, P], U8, align_bytes=64)
         width = GROUP * P * 2
         def first_matmul(grp):
             w_sb = live["w_sb", grp]
@@ -269,15 +267,11 @@ def tile_fourierkartlayer_k_kernel(tc, X0, t, Wc_w_words, Wc_w_scales, Wc_b, w, 
                 op1=ALU.subtract,
             )
 
-        def row_folds(grp):
-            row_a = rows.tile([P, HARM * width], F32, name="row_a", bufs=2)
-            y = live["row_y", grp][:, 0, :FOLD]
-            nc.vector.scalar_tensor_tensor(out=row_a[:, :FOLD], in0=y, scalar=-0.25, in1=y, op0=ALU.is_lt, op1=ALU.add)
-            live["row_a", grp] = row_a
-
         def row_magnitudes(grp):
-            y = live["row_y", grp][:].rearrange("p e c -> p (e c)")
-            nc.scalar.activation(out=live["row_a", grp][:, FOLD:], in_=y[:, FOLD:], func=ACT.Abs)
+            y = live["row_y", grp]
+            row_abs = rows.tile([P, HARM, width], F32, name="row_abs")
+            nc.scalar.activation(out=row_abs[:], in_=y[:], func=ACT.Abs)
+            live["row_abs", grp] = row_abs
 
         def row_sines(grp):
             y = live["row_y", grp]
@@ -293,18 +287,21 @@ def tile_fourierkartlayer_k_kernel(tc, X0, t, Wc_w_words, Wc_w_scales, Wc_b, w, 
         def row_cosines(grp):
             nc.scalar.activation(
                 out=live["row_bf", grp][:, 1, :].rearrange("p (c e) -> p c e", e=HARM),
-                in_=live["row_a", grp][:].rearrange("p (e c) -> p c e", e=HARM),
+                in_=live["row_abs", grp][:].rearrange("p e c -> p c e"),
                 func=ACT.Sin,
                 scale=-TWO_PI,
                 bias=HALF_PI,
             )
 
         def quantise_rows(grp):
+            row_codes = codes.tile([P, 2, GROUP, P], U32, align_bytes=64, name="row_codes")
+            row_scales = codes.tile([P, 2, GROUP, P], U8, align_bytes=64, name="row_scales")
             nc.vector.quantize_mx(
-                out=row_codes[:, grp, :, :, :].rearrange("p f g r -> p (f g r)").bitcast(FP8X4),
-                scales=row_scales[:, grp, :, :, :].rearrange("p f g r -> p (f g r)"),
+                out=row_codes[:].rearrange("p f g r -> p (f g r)").bitcast(FP8X4),
+                scales=row_scales[:].rearrange("p f g r -> p (f g r)"),
                 in_=live["row_bf", grp][:].rearrange("p f c -> p (f c)"),
             )
+            live["row_codes", grp] = (row_codes, row_scales)
 
         last = PASSES - 1
         acc = ps_acc.tile([P, D_OUT], F32)
@@ -351,8 +348,8 @@ def tile_fourierkartlayer_k_kernel(tc, X0, t, Wc_w_words, Wc_w_scales, Wc_b, w, 
 
         def quantise(g, f0, f1):
             if f0 == 0:
-                live["w_codes", g] = codes.tile([P, 2, D_OUT], U32, align_bytes=64, name="w_codes", bufs=3)
-                live["w_code_scales", g] = codes.tile([P, 2, D_OUT], U8, align_bytes=64, name="w_code_scales", bufs=3)
+                live["w_codes", g] = codes.tile([P, 2, D_OUT], U32, align_bytes=64, name="w_codes", bufs=5)
+                live["w_code_scales", g] = codes.tile([P, 2, D_OUT], U8, align_bytes=64, name="w_code_scales", bufs=5)
             nc.vector.quantize_mx(
                 out=live["w_codes", g][:, f0:f1, :].rearrange("p f d -> p (f d)").bitcast(FP8X4),
                 scales=live["w_code_scales", g][:, f0:f1, :].rearrange("p f d -> p (f d)"),
@@ -361,11 +358,12 @@ def tile_fourierkartlayer_k_kernel(tc, X0, t, Wc_w_words, Wc_w_scales, Wc_b, w, 
 
         def long_sum(g):
             grp, gl = divmod(g, GROUP)
+            row_codes, row_scales = live["row_codes", grp]
             for f in range(2):
                 nc.tensor.matmul_mx(
                     out=acc[:],
-                    lhsT=row_codes[:, grp, 1 - f, gl, :].bitcast(FP8X4),
-                    lhsT_scale=row_scales[:, grp, 1 - f, gl, :],
+                    lhsT=row_codes[:, 1 - f, gl, :].bitcast(FP8X4),
+                    lhsT_scale=row_scales[:, 1 - f, gl, :],
                     rhs=live["w_codes", g][:, f, :].bitcast(FP8X4),
                     rhs_scale=live["w_code_scales", g][:, f, :],
                     start=(g == 0 and f == 0),
@@ -373,70 +371,63 @@ def tile_fourierkartlayer_k_kernel(tc, X0, t, Wc_w_words, Wc_w_scales, Wc_b, w, 
                 )
 
         first_matmul(0)
-        row_angles(0)
-
-        def due(step, lead):
-            return [g for g in range(PASSES) if step + lead == (g - 1 if g < FIRST else g)]
-
-        for step in range(1 - ROWS_LEAD, PASSES):
+        for step in range(-ROWS_LEAD, PASSES):
 
             def row_stage(stage, steps, *more):
                 grp, rest = divmod(step + ROWS_LEAD - steps, GROUP)
                 if rest == 0 and 0 <= grp < GROUPS:
                     stage(grp, *more)
 
-            row_stage(load_w, -GROUP - 1)
-            if step + PREFETCH < PASSES:
+            row_stage(load_w, -3)
+            if FIRST <= step + PREFETCH < PASSES:
                 load_rows("bp_sb", bp_rows, step + PREFETCH)
                 load_rows("a_sb", a_rows, step + PREFETCH)
-            if step < 0:
-                for g in due(step, 2):
-                    if g > 0:
-                        reduce_phases(g)
-            row_stage(row_reduce, 2, 0)
-            row_stage(row_reduce, 3, 1)
-            row_stage(row_folds, 3)
-            row_stage(quantise_rows, 6)
+            if 0 <= step + 1 < PASSES:
+                phase_sines(step + 1, 0)
+            if step >= 0:
+                phase_cosines(step, 1)
+            row_stage(row_magnitudes, 5)
+            row_stage(row_sines, 5)
+            row_stage(row_cosines, 6)
+            if 0 <= step + 1 < PASSES:
+                phase_sines(step + 1, 1)
+                phase_cosines(step + 1, 0)
+            if step == 0:
+                for half in range(UNITS_PER_PASS):
+                    multiply(0, half, 0, 2)
+            row_stage(row_reduce, 4, 0)
+            row_stage(row_reduce, 4, 1)
+            row_stage(quantise_rows, 7)
             if step >= 1:
                 quantise(step - 1, 0, 2)
-            if step >= 0:
-                for g in due(step, 2):
-                    reduce_phases(g)
+            if 0 < step + 2 < PASSES:
+                reduce_phases(step + 2)
             if FIRST <= step + 3 < PASSES:
                 count_turns(step + 3)
             row_stage(row_turns, 1, 0)
             row_stage(row_turns, 2, 1)
-            for g in due(step, 1):
-                phase_sines(g, 0)
-            for g in due(step, 0):
-                phase_cosines(g, 1)
-            row_stage(row_magnitudes, 4)
-            row_stage(row_cosines, 5)
-            for g in due(step, 1):
-                phase_sines(g, 1)
-                phase_cosines(g, 0)
-            row_stage(row_sines, 4)
             for half in range(UNITS_PER_PASS):
-                for g in due(step, 2):
-                    if g > 0:
-                        transpose_y(g, half)
-                if 0 <= step < last:
+                if 0 < step + 2 < PASSES:
+                    transpose_y(step + 2, half)
+                if 0 < step < last:
                     multiply(step, half, 0, 2)
                 if half == 0:
                     row_stage(row_angles, 0)
                 if 0 <= step + 1 < PASSES:
                     transpose_a(step + 1, half)
-            if step >= 2:
-                long_sum(step - 2)
+            if step >= SUM_LAG:
+                long_sum(step - SUM_LAG)
             row_stage(first_matmul, -1)
+        row_magnitudes(GROUPS - 1)
+        row_sines(GROUPS - 1)
+        row_cosines(GROUPS - 1)
         for f in range(2):
             for half in range(UNITS_PER_PASS):
                 multiply(last, half, f, f + 1)
             quantise(last, f, f + 1)
-            if f == 0:
-                quantise_rows(GROUPS - 1)
-        long_sum(last - 1)
-        long_sum(last)
+            quantise_rows(GROUPS - 2 + f)
+        for g in range(PASSES - SUM_LAG, PASSES):
+            long_sum(g)
 
         result = keep.tile([P, D_OUT], F32)
         nc.vector.tensor_copy(out=result[:], in_=acc[:])

@@ -30,6 +30,7 @@ GROUP = 2
 GROUPS = PASSES // GROUP
 PAIR = 2
 UNITS_PER_PASS = D_BLOCKS // PAIR
+ROW_Q = GROUP * K_PASS // HARM
 WORDS = K_PASS // HARM
 
 PLAIN = 1
@@ -88,14 +89,14 @@ def tile_fourierkartlayer_k_kernel(tc, X0, t, Wc_w_words, Wc_w_scales, Wc_b, w, 
             nc.sync.dma_start(out=sb[:], in_=source[:, qk_cols].rearrange("(j p) c -> p j c", p=P))
             live[name, g] = sb
 
+        bw_rows = keep.tile([Q_BLOCKS, 2, P], BF16)
+        nc.sync.dma_start(out=bw_rows[:, 0, :], in_=Wc_b.rearrange("(j p) -> j p", p=P))
+        nc.sync.dma_start(out=bw_rows[:, 1, :], in_=w.rearrange("(j p) -> j p", p=P))
+        t_bf = keep.tile([Q_BLOCKS, 2], BF16)
+        nc.sync.dma_start(out=t_bf[:], in_=t.rearrange("b o -> (b o)").partition_broadcast(Q_BLOCKS))
         load_rows("bp_sb", bp_rows, 0)
         x0_sb = keep.tile([P, D_IN], BF16)
         nc.sync.dma_start(out=x0_sb[:], in_=x0_rows)
-        bw_rows = keep.tile([P, P], BF16)
-        nc.sync.dma_start(out=bw_rows[0:Q_BLOCKS, :], in_=Wc_b.rearrange("(j p) -> j p", p=P))
-        nc.sync.dma_start(out=bw_rows[Q_BLOCKS:P, :], in_=w.rearrange("(j p) -> j p", p=P))
-        t_bf = keep.tile([P, 2], BF16)
-        nc.sync.dma_start(out=t_bf[:], in_=t.rearrange("b o -> (b o)").partition_broadcast(P))
         for quad in range(4):
             nc.sync.dma_start(
                 out=w_scales[32 * quad : 32 * quad + 4, :].bitcast(I32),
@@ -107,10 +108,34 @@ def tile_fourierkartlayer_k_kernel(tc, X0, t, Wc_w_words, Wc_w_scales, Wc_b, w, 
             nc.sync.dma_start(out=w_sb[:].bitcast(I32), in_=w_words[:, grp * GROUP * 2 * P : (grp + 1) * GROUP * 2 * P])
             live["w_sb", grp] = w_sb
 
+        parked = out.rearrange("b s d -> b (s d)")[:, 0:Q]
+
+        def load_shift(grp):
+            shift = wload.tile([P, ROW_Q], F32, name="shift")
+            for b in range(2):
+                nc.sync.dma_start(
+                    out=shift[b * S_LEN : (b + 1) * S_LEN, :],
+                    in_=parked[b, grp * ROW_Q : (grp + 1) * ROW_Q].partition_broadcast(S_LEN),
+                )
+            live["shift", grp] = shift
+
         load_w(0)
         load_rows("bp_sb", bp_rows, 1)
+        shift_rows = keep.tile([Q_BLOCKS, 2, P], F32)
+        for b in range(2):
+            nc.vector.scalar_tensor_tensor(
+                out=shift_rows[:, b, :],
+                in0=bw_rows[:, 1, :],
+                scalar=t_bf[:, b : b + 1],
+                in1=bw_rows[:, 0, :],
+                op0=ALU.mult,
+                op1=ALU.add,
+            )
+        nc.sync.dma_start(out=parked.rearrange("b (j p) -> j b p", p=P), in_=shift_rows[:])
+        load_shift(0)
         load_rows("a_sb", a_rows, 0)
         load_w(1)
+        load_shift(1)
         load_rows("a_sb", a_rows, 1)
 
         def spans(g):
@@ -134,28 +159,43 @@ def tile_fourierkartlayer_k_kernel(tc, X0, t, Wc_w_words, Wc_w_scales, Wc_b, w, 
             live["turns", g] = turns
             live["wide", g] = wide
 
+        def folded(g):
+            return g % 2 == 0
+
         def reduce_phases(g):
             turns = live["turns", g]
             reduced = args.tile([P, D_BLOCKS, K_PASS], F32, name="reduced")
             live["reduced", g] = reduced
             for lo, hi in spans(g):
+                if hi == D_BLOCKS:
+                    nc.vector.scalar_tensor_tensor(
+                        out=reduced[:, SUMMED:, :],
+                        in0=turns[:, SUMMED:, :],
+                        scalar=-TWO_PI,
+                        in1=live["bp_sb", g][:, SUMMED:, :],
+                        op0=ALU.mult,
+                        op1=ALU.add,
+                    )
                 end = min(hi, SUMMED)
                 nc.vector.tensor_scalar(
                     out=reduced[:, lo:end, :], in0=turns[:, lo:end, :], scalar1=-TWO_PI, scalar2=None, op0=ALU.mult
                 )
-            nc.vector.scalar_tensor_tensor(
-                out=reduced[:, SUMMED:, :],
-                in0=turns[:, SUMMED:, :],
-                scalar=-TWO_PI,
-                in1=live["bp_sb", g][:, SUMMED:, :],
-                op0=ALU.mult,
-                op1=ALU.add,
-            )
+            if folded(g):
+                fold = args.tile([P, K_PASS], F32, name="fold")
+                nc.vector.tensor_scalar(
+                    out=fold[:],
+                    in0=reduced[:, D_BLOCKS - 1, :],
+                    scalar1=HALF_PI,
+                    scalar2=-TWO_PI,
+                    op0=ALU.is_gt,
+                    op1=ALU.mult,
+                )
+                live["fold", g] = fold
 
         def transpose_y(g, half):
             for j in range(PAIR):
                 block = half * PAIR + j
-                y_ps = ps_y.tile([P, P, PACK], F32, name="y_ps")
+                y_ps = ps_y.tile([P, P, PACK], F32, name="y_ps", tag="y_ps")
                 for u in range(2):
                     for e in range(HARM):
                         cols = slice(u * 2 * P + e, (u + 1) * 2 * P - 1 + e, 2)
@@ -188,6 +228,24 @@ def tile_fourierkartlayer_k_kernel(tc, X0, t, Wc_w_words, Wc_w_scales, Wc_b, w, 
                         )
                 live["y_ps", g, block] = y_ps
 
+        def transpose_fold(g):
+            block = D_BLOCKS - 1
+            fold_ps = ps_y.tile([P, P, PACK], F32, name="fold_ps", tag="y_ps")
+            for u in range(2):
+                for e in range(HARM):
+                    cols = slice(u * 2 * P + e, (u + 1) * 2 * P - 1 + e, 2)
+                    parts = (live["reduced", g][:, block, cols], live["fold", g][:, cols])
+                    for i, part in enumerate(parts):
+                        nc.tensor.matmul(
+                            out=fold_ps[:, :, 2 * u + e],
+                            lhsT=part,
+                            rhs=ident[:],
+                            is_transpose=True,
+                            start=(i == 0),
+                            stop=(i == 1),
+                        )
+            live["fold_ps", g] = fold_ps
+
         x0_words = x0_sb[:].bitcast(F32)
         x0_ps = ps_c.tile([P, P, 2], F32, tag="c")
         for u in range(2):
@@ -204,92 +262,72 @@ def tile_fourierkartlayer_k_kernel(tc, X0, t, Wc_w_words, Wc_w_scales, Wc_b, w, 
             transpose_y(0, half)
         count_turns(1)
 
-        bw_ps = ps_c.tile([P, P], BF16, tag="c")
-        nc.tensor.transpose(bw_ps[:], bw_rows[:], ident_bf[:])
-        b_cols = keep.tile([P, Q_BLOCKS], F32)
-        nc.vector.tensor_copy(out=b_cols[:], in_=bw_ps[:, 0:Q_BLOCKS])
-        shift = keep.tile([P, Q_BLOCKS, 2], F32)
-        for b in range(2):
-            nc.vector.scalar_tensor_tensor(
-                out=shift[:, :, b],
-                in0=bw_ps[:, Q_BLOCKS:P],
-                scalar=t_bf[:, b : b + 1],
-                in1=b_cols[:],
-                op0=ALU.mult,
-                op1=ALU.add,
-            )
-
-        width = GROUP * P * 2
         def first_matmul(grp):
-            w_sb = live["w_sb", grp]
-            c_ps = ps_c.tile([P, GROUP * 2, P], F32, name="c_ps", tag="c")
-            for blk in range(GROUP * 2):
-                q_cols = slice((grp * GROUP * 2 + blk) * P, (grp * GROUP * 2 + blk + 1) * P)
-                nc.tensor.matmul_mx(
-                    out=c_ps[:, blk, :],
-                    lhsT=w_sb[:, blk * P : (blk + 1) * P].bitcast(FP8X4),
-                    lhsT_scale=w_scales[:, q_cols],
-                    rhs=x0_codes[:].bitcast(FP8X4),
-                    rhs_scale=x0_scales[:],
-                    start=True,
-                    stop=True,
-                )
+            q_cols = slice(grp * ROW_Q, (grp + 1) * ROW_Q)
+            c_ps = ps_c.tile([P, ROW_Q], F32, name="c_ps", tag="c")
+            nc.tensor.matmul_mx(
+                out=c_ps[:],
+                lhsT=x0_codes[:].bitcast(FP8X4),
+                lhsT_scale=x0_scales[:],
+                rhs=live["w_sb", grp][:].bitcast(FP8X4),
+                rhs_scale=w_scales[:, q_cols],
+                start=True,
+                stop=True,
+            )
             live["c_ps", grp] = c_ps
 
         def row_angles(grp):
-            c_ps = live["c_ps", grp]
-            angle = rows.tile([P, GROUP, P * 2], F32, name="angle", bufs=2)
-            for gl in range(GROUP):
-                blocks = slice(grp * GROUP * 2 + 2 * gl, grp * GROUP * 2 + 2 * gl + 2)
-                nc.vector.tensor_tensor(
-                    out=angle[:, gl, :].rearrange("p (b r u) -> p b r u", b=2, u=2),
-                    in0=c_ps[:, 2 * gl : 2 * gl + 2, :].rearrange("p u (b r) -> p b r u", b=2),
-                    in1=shift[:, blocks, :].rearrange("p u b -> p b u").unsqueeze(2).to_broadcast([P, 2, S_LEN, 2]),
-                    op=ALU.add,
-                )
+            angle = rows.tile([P, ROW_Q], F32, name="angle", bufs=3)
+            nc.vector.tensor_tensor(out=angle[:], in0=live["c_ps", grp][:], in1=live["shift", grp][:], op=ALU.add)
             live["angle", grp] = angle
 
         def row_turns(grp, e):
             if e == 0:
-                live["row_turns", grp] = rows.tile([P, HARM, width], I32, name="row_turns", bufs=2)
-            angle = live["angle", grp][:].rearrange("p g c -> p (g c)")
-            whole_turns(nc, live["row_turns", grp][:, e, :], angle, (e + 1) / TWO_PI)
+                live["row_turns", grp] = rows.tile([P, HARM, ROW_Q], I32, name="row_turns", bufs=2)
+            whole_turns(nc, live["row_turns", grp][:, e, :], live["angle", grp][:], (e + 1) / TWO_PI)
 
-        def row_reduce(grp, e):
-            if e == 0:
-                live["row_y", grp] = rows.tile([P, HARM, width], F32, name="row_y", bufs=2)
-            nc.vector.scalar_tensor_tensor(
-                out=live["row_y", grp][:, e, :],
-                in0=live["angle", grp][:].rearrange("p g c -> p (g c)"),
-                scalar=(e + 1) / TWO_PI,
-                in1=live["row_turns", grp][:, e, :],
-                op0=ALU.mult,
-                op1=ALU.subtract,
+        def row_reduce(grp):
+            row_minus = rows.tile([P, HARM, ROW_Q], F32, name="row_minus")
+            nc.vector.tensor_scalar(
+                out=row_minus[:], in0=live["row_turns", grp][:], scalar1=-TWO_PI, scalar2=None, op0=ALU.mult
             )
+            live["row_minus", grp] = row_minus
 
-        def row_magnitudes(grp):
-            y = live["row_y", grp]
-            row_abs = rows.tile([P, HARM, width], F32, name="row_abs")
-            nc.scalar.activation(out=row_abs[:], in_=y[:], func=ACT.Abs)
-            live["row_abs", grp] = row_abs
+        def transpose_rows(grp):
+            angle = live["angle", grp]
+            for gl in range(GROUP):
+                row_ps = ps_y.tile([P, P, PACK], F32, name="row_ps", tag="y_ps")
+                for u in range(2):
+                    q_block = slice((2 * gl + u) * P, (2 * gl + u + 1) * P)
+                    for e in range(HARM):
+                        parts = [angle[:, q_block]] * (e + 1) + [live["row_minus", grp][:, e, q_block]]
+                        for i, part in enumerate(parts):
+                            nc.tensor.matmul(
+                                out=row_ps[:, :, 2 * u + e],
+                                lhsT=part,
+                                rhs=ident[:],
+                                is_transpose=True,
+                                start=(i == 0),
+                                stop=(i == e + 1),
+                            )
+                live["row_ps", grp, gl] = row_ps
 
         def row_sines(grp):
-            y = live["row_y", grp]
-            row_bf = rows.tile([P, 2, width * HARM], BF16, align_bytes=64, name="row_bf")
-            nc.scalar.activation(
-                out=row_bf[:, 0, :].rearrange("p (c e) -> p c e", e=HARM),
-                in_=y[:].rearrange("p e c -> p c e"),
-                func=ACT.Sin,
-                scale=TWO_PI,
-            )
+            row_bf = rows.tile([P, 2, GROUP, K_PASS], BF16, align_bytes=64, name="row_bf", bufs=2)
+            row_abs = rows.tile([P, GROUP, K_PASS], F32, name="row_abs")
+            for gl in range(GROUP):
+                flat = live["row_ps", grp, gl][:].rearrange("p r t -> p (r t)")
+                nc.scalar.activation(out=row_bf[:, 0, gl, :], in_=flat, func=ACT.Sin)
+                nc.scalar.activation(out=row_abs[:, gl, :], in_=flat, func=ACT.Abs)
             live["row_bf", grp] = row_bf
+            live["row_abs", grp] = row_abs
 
         def row_cosines(grp):
             nc.scalar.activation(
-                out=live["row_bf", grp][:, 1, :].rearrange("p (c e) -> p c e", e=HARM),
-                in_=live["row_abs", grp][:].rearrange("p e c -> p c e"),
+                out=live["row_bf", grp][:, 1, :, :],
+                in_=live["row_abs", grp][:],
                 func=ACT.Sin,
-                scale=-TWO_PI,
+                scale=-1.0,
                 bias=HALF_PI,
             )
 
@@ -299,7 +337,7 @@ def tile_fourierkartlayer_k_kernel(tc, X0, t, Wc_w_words, Wc_w_scales, Wc_b, w, 
             nc.vector.quantize_mx(
                 out=row_codes[:].rearrange("p f g r -> p (f g r)").bitcast(FP8X4),
                 scales=row_scales[:].rearrange("p f g r -> p (f g r)"),
-                in_=live["row_bf", grp][:].rearrange("p f c -> p (f c)"),
+                in_=live["row_bf", grp][:].rearrange("p f g c -> p (f g c)"),
             )
             live["row_codes", grp] = (row_codes, row_scales)
 
@@ -321,14 +359,19 @@ def tile_fourierkartlayer_k_kernel(tc, X0, t, Wc_w_words, Wc_w_scales, Wc_b, w, 
             for j in range(PAIR):
                 flat = live["y_ps", g, half * PAIR + j][:].rearrange("p d t -> p (d t)")
                 nc.scalar.activation(out=sin_cos[:, 0, j, :], in_=flat, func=ACT.Sin)
-                nc.scalar.activation(out=abs_b[:, j, :], in_=flat, func=ACT.Abs)
+                if folded(g) and half * PAIR + j == D_BLOCKS - 1:
+                    fold_flat = live["fold_ps", g][:].rearrange("p d t -> p (d t)")
+                    nc.scalar.activation(out=sin_cos[:, 1, j, :], in_=fold_flat, func=ACT.Sin, bias=HALF_PI)
+                else:
+                    nc.scalar.activation(out=abs_b[:, j, :], in_=flat, func=ACT.Abs)
             live["sin_cos", g, half] = sin_cos
             live["abs_b", g, half] = abs_b
 
         def phase_cosines(g, half):
+            blocks = slice(0, PAIR - 1 if folded(g) and half == UNITS_PER_PASS - 1 else PAIR)
             nc.scalar.activation(
-                out=live["sin_cos", g, half][:, 1, :, :],
-                in_=live["abs_b", g, half][:],
+                out=live["sin_cos", g, half][:, 1, blocks, :],
+                in_=live["abs_b", g, half][:, blocks, :],
                 func=ACT.Sin,
                 scale=-1.0,
                 bias=HALF_PI,
@@ -379,24 +422,27 @@ def tile_fourierkartlayer_k_kernel(tc, X0, t, Wc_w_words, Wc_w_scales, Wc_b, w, 
                     stage(grp, *more)
 
             row_stage(load_w, -3)
+            row_stage(load_shift, -3)
             if FIRST <= step + PREFETCH < PASSES:
                 load_rows("bp_sb", bp_rows, step + PREFETCH)
                 load_rows("a_sb", a_rows, step + PREFETCH)
+            row_stage(first_matmul, -1)
             if 0 <= step + 1 < PASSES:
                 phase_sines(step + 1, 0)
             if step >= 0:
                 phase_cosines(step, 1)
-            row_stage(row_magnitudes, 5)
-            row_stage(row_sines, 5)
+            row_stage(transpose_rows, 5)
             row_stage(row_cosines, 6)
             if 0 <= step + 1 < PASSES:
+                if folded(step + 1):
+                    transpose_fold(step + 1)
                 phase_sines(step + 1, 1)
                 phase_cosines(step + 1, 0)
+            row_stage(row_sines, 5)
             if step == 0:
                 for half in range(UNITS_PER_PASS):
                     multiply(0, half, 0, 2)
-            row_stage(row_reduce, 4, 0)
-            row_stage(row_reduce, 4, 1)
+            row_stage(row_reduce, 4)
             row_stage(quantise_rows, 7)
             if step >= 1:
                 quantise(step - 1, 0, 2)
@@ -417,8 +463,7 @@ def tile_fourierkartlayer_k_kernel(tc, X0, t, Wc_w_words, Wc_w_scales, Wc_b, w, 
                     transpose_a(step + 1, half)
             if step >= SUM_LAG:
                 long_sum(step - SUM_LAG)
-            row_stage(first_matmul, -1)
-        row_magnitudes(GROUPS - 1)
+        transpose_rows(GROUPS - 1)
         row_sines(GROUPS - 1)
         row_cosines(GROUPS - 1)
         for f in range(2):

@@ -47,8 +47,8 @@ HALF_PI = 0.5 * math.pi
 FLOPS = 2 * P * D_IN * Q + 2 * 2 * P * QK * D_OUT
 
 
-def whole_turns(nc, turns, x, factor):
-    nc.gpsimd.tensor_scalar(out=turns, in0=x, scalar1=factor, scalar2=0.0, op0=ALU.mult, op1=ALU.add)
+def whole_turns(engine, turns, x, factor):
+    engine.tensor_scalar(out=turns, in0=x, scalar1=factor, scalar2=0.0, op0=ALU.mult, op1=ALU.add)
 
 
 def tile_fourierkartlayer_k_kernel(tc, X0, t, Wc_w_words, Wc_w_scales, Wc_b, w, A, Bp, out):
@@ -139,14 +139,15 @@ def tile_fourierkartlayer_k_kernel(tc, X0, t, Wc_w_words, Wc_w_scales, Wc_b, w, 
         load_rows("a_sb", a_rows, 1)
 
         def spans(g):
-            return ((0, PAIR), (PAIR, D_BLOCKS)) if g == 0 else ((0, D_BLOCKS),)
+            return ((0, PAIR), (PAIR, D_BLOCKS)) if g < FIRST else ((0, D_BLOCKS),)
 
         def count_turns(g):
             phases = live["bp_sb", g]
             turns = handoff.tile([P, D_BLOCKS, K_PASS], I32, name="phase_turns")
             wide = args.tile([P, WIDE, K_PASS], F32, name="wide")
             for lo, hi in spans(g):
-                whole_turns(nc, turns[:, lo:hi, :], phases[:, lo:hi, :], 1.0 / TWO_PI)
+                engine = nc.vector if g == 1 else nc.gpsimd
+                whole_turns(engine, turns[:, lo:hi, :], phases[:, lo:hi, :], 1.0 / TWO_PI)
                 first, end = max(lo, PLAIN), min(hi, SUMMED)
                 nc.gpsimd.tensor_scalar(
                     out=wide[:, first - PLAIN : end - PLAIN, :],
@@ -160,7 +161,7 @@ def tile_fourierkartlayer_k_kernel(tc, X0, t, Wc_w_words, Wc_w_scales, Wc_b, w, 
             live["wide", g] = wide
 
         def folded(g):
-            return g % 2 == 0
+            return g % 4 == 2
 
         def reduce_phases(g):
             turns = live["turns", g]
@@ -284,7 +285,7 @@ def tile_fourierkartlayer_k_kernel(tc, X0, t, Wc_w_words, Wc_w_scales, Wc_b, w, 
         def row_turns(grp, e):
             if e == 0:
                 live["row_turns", grp] = rows.tile([P, HARM, ROW_Q], I32, name="row_turns", bufs=2)
-            whole_turns(nc, live["row_turns", grp][:, e, :], live["angle", grp][:], (e + 1) / TWO_PI)
+            whole_turns(nc.gpsimd, live["row_turns", grp][:, e, :], live["angle", grp][:], (e + 1) / TWO_PI)
 
         def row_reduce(grp):
             row_minus = rows.tile([P, HARM, ROW_Q], F32, name="row_minus")

import math
from contextlib import ExitStack

import concourse.mybir as mybir
from concourse.masks import make_identity

F32 = mybir.dt.float32
BF16 = mybir.dt.bfloat16
I32 = mybir.dt.int32
U32 = mybir.dt.uint32
U8 = mybir.dt.uint8
FP8X4 = mybir.dt.float8_e4m3fn_x4
ACT = mybir.ActivationFunctionType
ALU = mybir.AluOpType

P = 128
PACK = 4
K_PASS = P * PACK
D_IN = 512
Q = 8192
HARM = 2
QK = Q * HARM
D_OUT = 512
S_LEN = 64

Q_BLOCKS = Q // P
PASSES = QK // K_PASS
D_BLOCKS = D_OUT // P
GROUP = 2
GROUPS = PASSES // GROUP
PAIR = 2
UNITS_PER_PASS = D_BLOCKS // PAIR
ROW_Q = GROUP * K_PASS // HARM
WORDS = K_PASS // HARM

PLAIN = 1
WIDE = 2
SUMMED = PLAIN + WIDE
FIRST = 2
PREFETCH = 5
ROWS_LEAD = 3
SUM_LAG = 4

TWO_PI = 2.0 * math.pi
HALF_PI = 0.5 * math.pi

FLOPS = 2 * P * D_IN * Q + 2 * 2 * P * QK * D_OUT


def whole_turns(engine, turns, x, factor):
    engine.tensor_scalar(out=turns, in0=x, scalar1=factor, scalar2=0.0, op0=ALU.mult, op1=ALU.add)


def tile_fourierkartlayer_k_kernel(tc, X0, t, Wc_w_words, Wc_w_scales, Wc_b, w, A, Bp, out):
    nc = tc.nc
    x0_rows = X0.flatten_outer_dims()
    w_words = Wc_w_words[0].rearrange("p n t -> p (n t)").bitcast(I32)
    a_rows = A.rearrange("d q k -> d (q k)")
    bp_rows = Bp.rearrange("d q k -> d (q k)")

    with ExitStack() as stack:
        keep = stack.enter_context(tc.tile_pool(name="keep", bufs=1))
        wload = stack.enter_context(tc.tile_pool(name="wload", bufs=2))
        rows = stack.enter_context(tc.tile_pool(name="rows", bufs=1))
        load = stack.enter_context(tc.tile_pool(name="load", bufs=5))
        handoff = stack.enter_context(tc.tile_pool(name="handoff", bufs=1))
        args = stack.enter_context(tc.tile_pool(name="args", bufs=2))
        trig = stack.enter_context(tc.tile_pool(name="trig", bufs=2))
        codes = stack.enter_context(tc.tile_pool(name="codes", bufs=2))
        ps_acc = stack.enter_context(tc.psum_pool(name="ps_acc", bufs=1))
        ps_a = stack.enter_context(tc.psum_pool(name="ps_a", bufs=2))
        ps_y = stack.enter_context(tc.psum_pool(name="ps_y", bufs=4))
        ps_c = stack.enter_context(tc.psum_pool(name="ps_c", bufs=1))
        stack.enter_context(tc.manual_schedule())

        ident = keep.tile([P, P], F32)
        make_identity(nc, ident[:])
        ident_bf = keep.tile([P, P], BF16)
        make_identity(nc, ident_bf[:])

        w_scales = keep.tile([P, Q], U8, align_bytes=64)
        nc.vector.memset(w_scales[:].bitcast(I32), 0)

        live = {}

        def load_rows(name, source, g):
            sb = load.tile([P, D_BLOCKS, K_PASS], BF16, name=name)
            qk_cols = slice(g * K_PASS, (g + 1) * K_PASS)
            nc.sync.dma_start(out=sb[:], in_=source[:, qk_cols].rearrange("(j p) c -> p j c", p=P))
            live[name, g] = sb

        bw_rows = keep.tile([Q_BLOCKS, 2, P], BF16)
        nc.sync.dma_start(out=bw_rows[:, 0, :], in_=Wc_b.rearrange("(j p) -> j p", p=P))
        nc.sync.dma_start(out=bw_rows[:, 1, :], in_=w.rearrange("(j p) -> j p", p=P))
        t_bf = keep.tile([Q_BLOCKS, 2], BF16)
        nc.sync.dma_start(out=t_bf[:], in_=t.rearrange("b o -> (b o)").partition_broadcast(Q_BLOCKS))
        load_rows("bp_sb", bp_rows, 0)
        x0_sb = keep.tile([P, D_IN], BF16)
        nc.sync.dma_start(out=x0_sb[:], in_=x0_rows)
        for quad in range(4):
            nc.sync.dma_start(
                out=w_scales[32 * quad : 32 * quad + 4, :].bitcast(I32),
                in_=Wc_w_scales[0, 4 * quad : 4 * quad + 4, :].bitcast(I32),
            )

        def load_w(grp):
            w_sb = wload.tile([P, GROUP * 2 * P], U32, align_bytes=64, name="w_sb")
            nc.sync.dma_start(out=w_sb[:].bitcast(I32), in_=w_words[:, grp * GROUP * 2 * P : (grp + 1) * GROUP * 2 * P])
            live["w_sb", grp] = w_sb

        parked = out.rearrange("b s d -> b (s d)")[:, 0:Q]

        def load_shift(grp):
            shift = wload.tile([P, ROW_Q], F32, name="shift")
            for b in range(2):
                nc.sync.dma_start(
                    out=shift[b * S_LEN : (b + 1) * S_LEN, :],
                    in_=parked[b, grp * ROW_Q : (grp + 1) * ROW_Q].partition_broadcast(S_LEN),
                )
            live["shift", grp] = shift

        load_w(0)
        load_rows("bp_sb", bp_rows, 1)
        shift_rows = keep.tile([Q_BLOCKS, 2, P], F32)
        for b in range(2):
            nc.vector.scalar_tensor_tensor(
                out=shift_rows[:, b, :],
                in0=bw_rows[:, 1, :],
                scalar=t_bf[:, b : b + 1],
                in1=bw_rows[:, 0, :],
                op0=ALU.mult,
                op1=ALU.add,
            )
        nc.sync.dma_start(out=parked.rearrange("b (j p) -> j b p", p=P), in_=shift_rows[:])
        load_shift(0)
        load_rows("a_sb", a_rows, 0)
        load_w(1)
        load_shift(1)
        load_rows("a_sb", a_rows, 1)

        def spans(g):
            return ((0, PAIR), (PAIR, D_BLOCKS)) if g < FIRST else ((0, D_BLOCKS),)

        def count_turns(g):
            phases = live["bp_sb", g]
            turns = handoff.tile([P, D_BLOCKS, K_PASS], I32, name="phase_turns")
            wide = args.tile([P, WIDE, K_PASS], F32, name="wide")
            for lo, hi in spans(g):
                engine = nc.vector if g == 1 else nc.gpsimd
                whole_turns(engine, turns[:, lo:hi, :], phases[:, lo:hi, :], 1.0 / TWO_PI)
                first, end = max(lo, PLAIN), min(hi, SUMMED)
                nc.gpsimd.tensor_scalar(
                    out=wide[:, first - PLAIN : end - PLAIN, :],
                    in0=phases[:, first:end, :],
                    scalar1=1.0,
                    scalar2=0.0,
                    op0=ALU.mult,
                    op1=ALU.add,
                )
            live["turns", g] = turns
            live["wide", g] = wide

        def folded(g):
            return g % 4 == 2

        def reduce_phases(g):
            turns = live["turns", g]
            reduced = args.tile([P, D_BLOCKS, K_PASS], F32, name="reduced")
            live["reduced", g] = reduced
            for lo, hi in spans(g):
                if hi == D_BLOCKS:
                    nc.vector.scalar_tensor_tensor(
                        out=reduced[:, SUMMED:, :],
                        in0=turns[:, SUMMED:, :],
                        scalar=-TWO_PI,
                        in1=live["bp_sb", g][:, SUMMED:, :],
                        op0=ALU.mult,
                        op1=ALU.add,
                    )
                end = min(hi, SUMMED)
                nc.vector.tensor_scalar(
                    out=reduced[:, lo:end, :], in0=turns[:, lo:end, :], scalar1=-TWO_PI, scalar2=None, op0=ALU.mult
                )
            if folded(g):
                fold = args.tile([P, K_PASS], F32, name="fold")
                nc.vector.tensor_scalar(
                    out=fold[:],
                    in0=reduced[:, D_BLOCKS - 1, :],
                    scalar1=HALF_PI,
                    scalar2=-TWO_PI,
                    op0=ALU.is_gt,
                    op1=ALU.mult,
                )
                live["fold", g] = fold

        def transpose_y(g, half):
            for j in range(PAIR):
                block = half * PAIR + j
                y_ps = ps_y.tile([P, P, PACK], F32, name="y_ps", tag="y_ps")
                for u in range(2):
                    for e in range(HARM):
                        cols = slice(u * 2 * P + e, (u + 1) * 2 * P - 1 + e, 2)
                        y_block = y_ps[:, :, 2 * u + e]
                        alone = block >= SUMMED
                        if block < PLAIN:
                            nc.tensor.matmul(
                                out=y_block,
                                lhsT=live["bp_sb", g][:, block, cols],
                                rhs=ident_bf[:],
                                start=True,
                                stop=False,
                            )
                        elif not alone:
                            nc.tensor.matmul(
                                out=y_block,
                                lhsT=live["wide", g][:, block - PLAIN, cols],
                                rhs=ident[:],
                                is_transpose=True,
                                start=True,
                                stop=False,
                            )
                        nc.tensor.matmul(
                            out=y_block,
                            lhsT=live["reduced", g][:, block, cols],
                            rhs=ident[:],
                            is_transpose=True,
                            start=alone,
                            stop=True,
                        )
                live["y_ps", g, block] = y_ps

        def transpose_fold(g):
            block = D_BLOCKS - 1
            fold_ps = ps_y.tile([P, P, PACK], F32, name="fold_ps", tag="y_ps")
            for u in range(2):
                for e in range(HARM):
                    cols = slice(u * 2 * P + e, (u + 1) * 2 * P - 1 + e, 2)
                    parts = (live["reduced", g][:, block, cols], live["fold", g][:, cols])
                    for i, part in enumerate(parts):
                        nc.tensor.matmul(
                            out=fold_ps[:, :, 2 * u + e],
                            lhsT=part,
                            rhs=ident[:],
                            is_transpose=True,
                            start=(i == 0),
                            stop=(i == 1),
                        )
            live["fold_ps", g] = fold_ps

        x0_words = x0_sb[:].bitcast(F32)
        x0_ps = ps_c.tile([P, P, 2], F32, tag="c")
        for u in range(2):
            nc.tensor.transpose(x0_ps[:, :, u], x0_words[:, u : D_IN // 2 : 2], ident[:])
        x0_grouped = keep.tile([P, P * PACK], BF16, align_bytes=64)
        nc.vector.tensor_copy(out=x0_grouped[:].bitcast(F32), in_=x0_ps[:].rearrange("p r u -> p (r u)"))
        x0_codes = keep.tile([P, P], U32, align_bytes=64)
        x0_scales = keep.tile([P, P], U8, align_bytes=64)
        nc.vector.quantize_mx(out=x0_codes[:].bitcast(FP8X4), scales=x0_scales[:], in_=x0_grouped[:])

        count_turns(0)
        reduce_phases(0)
        for half in range(UNITS_PER_PASS):
            transpose_y(0, half)
        count_turns(1)

        def first_matmul(grp):
            q_cols = slice(grp * ROW_Q, (grp + 1) * ROW_Q)
            c_ps = ps_c.tile([P, ROW_Q], F32, name="c_ps", tag="c")
            nc.tensor.matmul_mx(
                out=c_ps[:],
                lhsT=x0_codes[:].bitcast(FP8X4),
                lhsT_scale=x0_scales[:],
                rhs=live["w_sb", grp][:].bitcast(FP8X4),
                rhs_scale=w_scales[:, q_cols],
                start=True,
                stop=True,
            )
            live["c_ps", grp] = c_ps

        def row_angles(grp):
            angle = rows.tile([P, ROW_Q], F32, name="angle", bufs=3)
            nc.vector.tensor_tensor(out=angle[:], in0=live["c_ps", grp][:], in1=live["shift", grp][:], op=ALU.add)
            live["angle", grp] = angle

        def row_turns(grp, e):
            if e == 0:
                live["row_turns", grp] = rows.tile([P, HARM, ROW_Q], I32, name="row_turns", bufs=2)
            whole_turns(nc.gpsimd, live["row_turns", grp][:, e, :], live["angle", grp][:], (e + 1) / TWO_PI)

        def row_reduce(grp):
            row_minus = rows.tile([P, HARM, ROW_Q], F32, name="row_minus")
            nc.vector.tensor_scalar(
                out=row_minus[:], in0=live["row_turns", grp][:], scalar1=-TWO_PI, scalar2=None, op0=ALU.mult
            )
            live["row_minus", grp] = row_minus

        def transpose_rows(grp):
            angle = live["angle", grp]
            for gl in range(GROUP):
                row_ps = ps_y.tile([P, P, PACK], F32, name="row_ps", tag="y_ps")
                for u in range(2):
                    q_block = slice((2 * gl + u) * P, (2 * gl + u + 1) * P)
                    for e in range(HARM):
                        parts = [angle[:, q_block]] * (e + 1) + [live["row_minus", grp][:, e, q_block]]
                        for i, part in enumerate(parts):
                            nc.tensor.matmul(
                                out=row_ps[:, :, 2 * u + e],
                                lhsT=part,
                                rhs=ident[:],
                                is_transpose=True,
                                start=(i == 0),
                                stop=(i == e + 1),
                            )
                live["row_ps", grp, gl] = row_ps

        def row_sines(grp):
            row_bf = rows.tile([P, 2, GROUP, K_PASS], BF16, align_bytes=64, name="row_bf", bufs=2)
            row_abs = rows.tile([P, GROUP, K_PASS], F32, name="row_abs")
            for gl in range(GROUP):
                flat = live["row_ps", grp, gl][:].rearrange("p r t -> p (r t)")
                nc.scalar.activation(out=row_bf[:, 0, gl, :], in_=flat, func=ACT.Sin)
                nc.scalar.activation(out=row_abs[:, gl, :], in_=flat, func=ACT.Abs)
            live["row_bf", grp] = row_bf
            live["row_abs", grp] = row_abs

        def row_cosines(grp):
            nc.scalar.activation(
                out=live["row_bf", grp][:, 1, :, :],
                in_=live["row_abs", grp][:],
                func=ACT.Sin,
                scale=-1.0,
                bias=HALF_PI,
            )

        def quantise_rows(grp):
            row_codes = codes.tile([P, 2, GROUP, P], U32, align_bytes=64, name="row_codes")
            row_scales = codes.tile([P, 2, GROUP, P], U8, align_bytes=64, name="row_scales")
            nc.vector.quantize_mx(
                out=row_codes[:].rearrange("p f g r -> p (f g r)").bitcast(FP8X4),
                scales=row_scales[:].rearrange("p f g r -> p (f g r)"),
                in_=live["row_bf", grp][:].rearrange("p f g c -> p (f g c)"),
            )
            live["row_codes", grp] = (row_codes, row_scales)

        last = PASSES - 1
        acc = ps_acc.tile([P, D_OUT], F32)

        def transpose_a(g, half):
            a_words = live["a_sb", g][:].rearrange("p j c -> p (j c)").bitcast(F32)
            a_ps = ps_a.tile([P, PAIR, P, 2], F32, name="a_ps")
            for j in range(PAIR):
                for u in range(2):
                    m0 = (half * PAIR + j) * WORDS + u * P
                    nc.tensor.transpose(a_ps[:, j, :, u], a_words[:, m0 : m0 + P], ident[:])
            live["a_ps", g, half] = a_ps

        def phase_sines(g, half):
            sin_cos = trig.tile([P, 2, PAIR, K_PASS], F32, name="sin_cos", bufs=4)
            abs_b = trig.tile([P, PAIR, K_PASS], F32, name="abs_b")
            for j in range(PAIR):
                flat = live["y_ps", g, half * PAIR + j][:].rearrange("p d t -> p (d t)")
                nc.scalar.activation(out=sin_cos[:, 0, j, :], in_=flat, func=ACT.Sin)
                if folded(g) and half * PAIR + j == D_BLOCKS - 1:
                    fold_flat = live["fold_ps", g][:].rearrange("p d t -> p (d t)")
                    nc.scalar.activation(out=sin_cos[:, 1, j, :], in_=fold_flat, func=ACT.Sin, bias=HALF_PI)
                else:
                    nc.scalar.activation(out=abs_b[:, j, :], in_=flat, func=ACT.Abs)
            live["sin_cos", g, half] = sin_cos
            live["abs_b", g, half] = abs_b

        def phase_cosines(g, half):
            blocks = slice(0, PAIR - 1 if folded(g) and half == UNITS_PER_PASS - 1 else PAIR)
            nc.scalar.activation(
                out=live["sin_cos", g, half][:, 1, blocks, :],
                in_=live["abs_b", g, half][:, blocks, :],
                func=ACT.Sin,
                scale=-1.0,
                bias=HALF_PI,
            )

        def multiply(g, half, f0, f1):
            a_t = live["a_ps", g, half][:].rearrange("p j d u -> p (j d u)").bitcast(BF16)
            if half == 0 and f0 == 0:
                live["products", g] = trig.tile([P, 2, D_BLOCKS * K_PASS], BF16, align_bytes=64, name="products")
            unit_cols = slice(half * PAIR * K_PASS, (half + 1) * PAIR * K_PASS)
            nc.vector.tensor_tensor(
                out=live["products", g][:, f0:f1, unit_cols],
                in0=live["sin_cos", g, half][:, f0:f1, :, :].rearrange("p f j c -> p f (j c)"),
                in1=a_t.unsqueeze(1).to_broadcast([P, f1 - f0, PAIR * K_PASS]),
                op=ALU.mult,
            )

        def quantise(g, f0, f1):
            if f0 == 0:
                live["w_codes", g] = codes.tile([P, 2, D_OUT], U32, align_bytes=64, name="w_codes", bufs=5)
                live["w_code_scales", g] = codes.tile([P, 2, D_OUT], U8, align_bytes=64, name="w_code_scales", bufs=5)
            nc.vector.quantize_mx(
                out=live["w_codes", g][:, f0:f1, :].rearrange("p f d -> p (f d)").bitcast(FP8X4),
                scales=live["w_code_scales", g][:, f0:f1, :].rearrange("p f d -> p (f d)"),
                in_=live["products", g][:, f0:f1, :].rearrange("p f c -> p (f c)"),
            )

        def long_sum(g):
            grp, gl = divmod(g, GROUP)
            row_codes, row_scales = live["row_codes", grp]
            for f in range(2):
                nc.tensor.matmul_mx(
                    out=acc[:],
                    lhsT=row_codes[:, 1 - f, gl, :].bitcast(FP8X4),
                    lhsT_scale=row_scales[:, 1 - f, gl, :],
                    rhs=live["w_codes", g][:, f, :].bitcast(FP8X4),
                    rhs_scale=live["w_code_scales", g][:, f, :],
                    start=(g == 0 and f == 0),
                    stop=(g == last and f == 1),
                )

        first_matmul(0)
        for step in range(-ROWS_LEAD, PASSES):

            def row_stage(stage, steps, *more):
                grp, rest = divmod(step + ROWS_LEAD - steps, GROUP)
                if rest == 0 and 0 <= grp < GROUPS:
                    stage(grp, *more)

            row_stage(load_w, -3)
            row_stage(load_shift, -3)
            if FIRST <= step + PREFETCH < PASSES:
                load_rows("bp_sb", bp_rows, step + PREFETCH)
                load_rows("a_sb", a_rows, step + PREFETCH)
            row_stage(first_matmul, -1)
            if 0 <= step + 1 < PASSES:
                phase_sines(step + 1, 0)
            if step >= 0:
                phase_cosines(step, 1)
            row_stage(transpose_rows, 5)
            row_stage(row_cosines, 6)
            if 0 <= step + 1 < PASSES:
                if folded(step + 1):
                    transpose_fold(step + 1)
                phase_sines(step + 1, 1)
                phase_cosines(step + 1, 0)
            row_stage(row_sines, 5)
            if step == 0:
                for half in range(UNITS_PER_PASS):
                    multiply(0, half, 0, 2)
            row_stage(row_reduce, 4)
            row_stage(quantise_rows, 7)
            if step >= 1:
                quantise(step - 1, 0, 2)
            if 0 < step + 2 < PASSES:
                reduce_phases(step + 2)
            if FIRST <= step + 3 < PASSES:
                count_turns(step + 3)
            row_stage(row_turns, 1, 0)
            row_stage(row_turns, 2, 1)
            for half in range(UNITS_PER_PASS):
                if 0 < step + 2 < PASSES:
                    transpose_y(step + 2, half)
                if 0 < step < last:
                    multiply(step, half, 0, 2)
                if half == 0:
                    row_stage(row_angles, 0)
                if 0 <= step + 1 < PASSES:
                    transpose_a(step + 1, half)
            if step >= SUM_LAG:
                long_sum(step - SUM_LAG)
        transpose_rows(GROUPS - 1)
        row_sines(GROUPS - 1)
        row_cosines(GROUPS - 1)
        for f in range(2):
            for half in range(UNITS_PER_PASS):
                multiply(last, half, f, f + 1)
            quantise(last, f, f + 1)
            quantise_rows(GROUPS - 2 + f)
        for g in range(PASSES - SUM_LAG, PASSES):
            long_sum(g)

        result = keep.tile([P, D_OUT], F32)
        nc.vector.tensor_copy(out=result[:], in_=acc[:])
        nc.sync.dma_start(out=out.flatten_outer_dims(), in_=result[:])
